import numpy as np
import ml_dtypes


def mxq(x, axis, fmt="e4m3"):
    dtype, down = {"e4m3": (ml_dtypes.float8_e4m3fn, 7), "e5m2": (ml_dtypes.float8_e5m2, 14)}[fmt]
    v = np.moveaxis(np.asarray(x, np.float32).astype(ml_dtypes.bfloat16).astype(np.float64), axis, -1)
    blocks = v.reshape(v.shape[:-1] + (-1, 32))
    amax = np.abs(blocks).max(-1, keepdims=True)
    byte = np.maximum(np.where(amax > 0, np.frexp(amax)[1] - 1 + 127, 0) - down, 1)
    scale = np.exp2(byte - 127.0)
    codes = (blocks / scale).astype(np.float32).astype(dtype).astype(np.float64)
    return np.moveaxis((codes * scale).reshape(v.shape), -1, axis)


WIDE = False


def mx_kscale(k):
    if not WIDE:
        return np.ones(k)
    levels = np.array([10, -10, 5, -5, 0])
    if k % 512:
        return np.exp2(np.random.permutation(np.resize(levels, k // 32))).repeat(32)
    a = np.empty((k // 512, 16))
    for p in range(k // 512):
        a[p, :8] = np.random.permutation(np.resize(levels, 8))
        for g in range(8):
            far = levels[np.abs(levels - a[p, g]) >= 10]
            a[p, g + 8] = far[np.random.randint(len(far))]
    return np.exp2(a.ravel()).repeat(32)


BF16 = ml_dtypes.bfloat16


def bf(x):
    return np.asarray(x, np.float32).astype(BF16)


def f64(x):
    return np.asarray(x).astype(np.float64)


N, K, D_IN, HC, H = 1024, 8, 512, 512, 1024


def sigmoid(v):
    return 1.0 / (1.0 + np.exp(-v))


def setup_inputs():
    s, t = mx_kscale(D_IN), mx_kscale(HC)
    return {
        "x": bf(np.random.standard_normal((N, D_IN)) * s),
        "child_h": bf(np.random.standard_normal((N, K, HC)) * t),
        "child_c": bf(np.random.standard_normal((N, K, H)) * 0.5),
        "Wf": bf(np.random.standard_normal((D_IN, H)) * 0.7 / np.sqrt(D_IN) / s[:, None]),
        "bWf": bf(np.random.standard_normal(H) * 0.3),
        "Uf": bf(np.random.standard_normal((HC, H)) * 0.7 / np.sqrt(HC) / t[:, None]),
        "bUf": bf(np.random.standard_normal(H) * 0.3),
    }


def reference(x, child_h, child_c, Wf, bWf, Uf, bUf):
    xf = (mxq(f64(x), 1, "e4m3") @ mxq(f64(Wf), 0, "e4m3")) + f64(bWf)
    hf = mxq(f64(child_h), 2, "e4m3") @ mxq(f64(Uf), 0, "e4m3")
    f = sigmoid(xf[:, None, :] + hf + f64(bUf))
    return (f * f64(child_c)).sum(axis=1)

@@ -1,0 +1,301 @@
+from contextlib import ExitStack
+
+import concourse.mybir as mybir
+from concourse.masks import make_identity
+
+F32 = mybir.dt.float32
+BF16 = mybir.dt.bfloat16
+U32 = mybir.dt.uint32
+U8 = mybir.dt.uint8
+FP8X4 = mybir.dt.float8_e4m3fn_x4
+SIGMOID = mybir.ActivationFunctionType.Sigmoid
+MULT = mybir.AluOpType.mult
+ADD = mybir.AluOpType.add
+
+P = 128
+PACK = 4
+NODES, CHILDREN, FEATURES, HIDDEN = 1024, 8, 512, 1024
+FLOPS = 2 * (NODES * CHILDREN + NODES) * FEATURES * HIDDEN
+
+NODE_BLOCK = 512
+BLOCKS = NODES // NODE_BLOCK
+TILES = NODE_BLOCK // P
+PAIR = 2
+WORDS = FEATURES // PAIR
+HALVES = WORDS // P
+H_BLOCK = PAIR * P
+H_BLOCKS = HIDDEN // H_BLOCK
+W_PARTS = 2
+W_PART = HIDDEN // W_PARTS
+STEPS = BLOCKS * CHILDREN
+AHEAD = 3
+LEAD = 2
+X_STEP = 2
+BLOCK_COLUMNS = PAIR * NODE_BLOCK
+STEP_COLUMNS = H_BLOCKS * BLOCK_COLUMNS
+GPSIMD_COLUMNS = BLOCK_COLUMNS
+
+
+def tile_childsumtreelstmcell_pa_t_kernel(tc, x, child_h, child_c, Wf, bWf, Uf, bUf, out):
+    nc = tc.nc
+    x_view = x.rearrange("(b p t) d -> b p (t d)", b=BLOCKS, t=TILES)
+    h_view = child_h.rearrange("(b p t) k d -> b p t k d", b=BLOCKS, t=TILES)
+    c_view = child_c.rearrange("(b p t) k h -> b p t k h", b=BLOCKS, t=TILES)
+    out_view = out.rearrange("(b p t) h -> b p t h", b=BLOCKS, t=TILES)
+
+    with ExitStack() as ctx:
+        const = ctx.enter_context(tc.tile_pool(name="const", bufs=1))
+        weights = ctx.enter_context(tc.tile_pool(name="weights", bufs=1))
+        wstage = ctx.enter_context(tc.tile_pool(name="wstage", bufs=2))
+        x_rows_pool = ctx.enter_context(tc.tile_pool(name="x_rows", bufs=BLOCKS))
+        h_rows_pool = ctx.enter_context(tc.tile_pool(name="h_rows", bufs=AHEAD))
+        c_rows_pool = ctx.enter_context(tc.tile_pool(name="c_rows", bufs=AHEAD + 1))
+        grouped_pool = ctx.enter_context(tc.tile_pool(name="grouped", bufs=3))
+        codes_pool = ctx.enter_context(tc.tile_pool(name="codes", bufs=LEAD + 1))
+        gate_pool = ctx.enter_context(tc.tile_pool(name="gate", bufs=6))
+        prod_pool = ctx.enter_context(tc.tile_pool(name="prod", bufs=2))
+        sum_pool = ctx.enter_context(tc.tile_pool(name="sums", bufs=2))
+        out_pool = ctx.enter_context(tc.tile_pool(name="out_rows", bufs=H_BLOCKS))
+        z_psum = ctx.enter_context(tc.psum_pool(name="z_psum", bufs=3))
+        c_psum = ctx.enter_context(tc.psum_pool(name="c_psum", bufs=3))
+        t_psum = ctx.enter_context(tc.psum_pool(name="t_psum", bufs=2))
+        ctx.enter_context(tc.manual_schedule())
+
+        def load_weight_part(w, name, part):
+            raw = weights.tile([P, PACK * W_PART], BF16, name="raw", tag="raw_%s%d" % (name, part))
+            nc.sync.dma_start(
+                out=raw[:].rearrange("q (j c) -> q j c", j=PACK),
+                in_=w[:, W_PART * part : W_PART * (part + 1)].rearrange("(q j) c -> q j c", j=PACK),
+            )
+            return raw
+
+        def regroup_weight_block(raw_parts, hb):
+            part, first = divmod(H_BLOCK * hb, W_PART)
+            grouped_w = wstage.tile([P, H_BLOCK * PACK], BF16, align_bytes=64)
+            nc.vector.tensor_copy(
+                out=grouped_w[:].rearrange("q (e m j) -> q e m j", e=PAIR, j=PACK),
+                in_=raw_parts[part][:].rearrange("q (j c) -> q j c", j=PACK)[:, :, first : first + H_BLOCK].rearrange(
+                    "q j (m e) -> q e m j", e=PAIR
+                ),
+            )
+            return grouped_w
+
+        def quantise_weight_blocks(hb):
+            cols = slice(H_BLOCK * hb, H_BLOCK * (hb + 1))
+            grouped_u = regroup_weight_block(u_raw, hb)
+            grouped_w = regroup_weight_block(w_raw, hb)
+            nc.vector.quantize_mx(out=u_codes[:, cols].bitcast(FP8X4), scales=u_scales[:, cols], in_=grouped_u[:])
+            nc.vector.quantize_mx(out=w_codes[:, cols].bitcast(FP8X4), scales=w_scales[:, cols], in_=grouped_w[:])
+
+        def load_x(b):
+            rows = x_rows_pool.tile([P, TILES * FEATURES], BF16, name="x_rows")
+            nc.sync.dma_start(out=rows[:], in_=x_view[b])
+            return rows
+
+        def load_children(s):
+            b, k = divmod(s, CHILDREN)
+            rows = h_rows_pool.tile([P, TILES * FEATURES], BF16, name="h_rows")
+            nc.sync.dma_start(out=rows[:].rearrange("p (t d) -> p t d", t=TILES), in_=h_view[b, :, :, k, :])
+            return rows
+
+        def load_cells(s):
+            b, k = divmod(s, CHILDREN)
+            rows = c_rows_pool.tile([P, TILES * HIDDEN], BF16, name="c_rows")
+            nc.sync.dma_start(out=rows[:].rearrange("p (t h) -> p t h", t=TILES), in_=c_view[b, :, :, k, :])
+            return rows
+
+        def transpose_rows(rows):
+            words = rows[:].bitcast(F32)
+            banks = []
+            for half in range(TILES // 2):
+                bank = t_psum.tile([P, 2, HALVES, P], F32, name="bank", tag="t")
+                for a in range(2):
+                    for u in range(HALVES):
+                        first = (2 * half + a) * WORDS
+                        nc.tensor.transpose(bank[:, a, u, :], words[:, first + u : first + WORDS : HALVES], ident[:])
+                banks.append(bank)
+            return banks
+
+        def regroup_rows(banks):
+            grouped = grouped_pool.tile([P, NODE_BLOCK * PACK], BF16, align_bytes=64)
+            grouped_words = grouped[:].bitcast(F32).rearrange("p (h a n u) -> p h a n u", h=2, a=2, u=HALVES)
+            for half in range(TILES // 2):
+                nc.scalar.copy(out=grouped_words[:, half], in_=banks[half][:].rearrange("p a u n -> p a n u"))
+            return grouped
+
+        def quantise_rows(grouped, kind):
+            codes = codes_pool.tile([P, NODE_BLOCK], U32, name="codes", tag="%s_codes" % kind, align_bytes=64)
+            scales = codes_pool.tile([P, NODE_BLOCK], U8, name="scales", tag="%s_scales" % kind, align_bytes=64)
+            nc.vector.quantize_mx(out=codes[:].bitcast(FP8X4), scales=scales[:], in_=grouped[:])
+            return codes, scales
+
+        def gate_sums(hb, e, child, node):
+            z = z_psum.tile([P, NODE_BLOCK], F32)
+            cols = slice((PAIR * hb + e) * P, (PAIR * hb + e + 1) * P)
+            nc.tensor.matmul_mx(
+                out=z[:],
+                lhsT=u_codes[:, cols].bitcast(FP8X4),
+                lhsT_scale=u_scales[:, cols],
+                rhs=child[0][:].bitcast(FP8X4),
+                rhs_scale=child[1][:],
+                start=True,
+                stop=False,
+            )
+            nc.tensor.matmul_mx(
+                out=z[:],
+                lhsT=w_codes[:, cols].bitcast(FP8X4),
+                lhsT_scale=w_scales[:, cols],
+                rhs=node[0][:].bitcast(FP8X4),
+                rhs_scale=node[1][:],
+                start=False,
+                stop=True,
+            )
+            return z
+
+        def transpose_cells(rows, hb):
+            words = rows[:].bitcast(F32)
+            cells = c_psum.tile([P, NODE_BLOCK], F32)
+            for t in range(TILES):
+                first = t * (HIDDEN // PAIR) + hb * P
+                nc.tensor.transpose(cells[:, t * P : (t + 1) * P], words[:, first : first + P], ident[:])
+            return cells
+
+        def store_block(b, hb):
+            total = sums[b][:, hb * BLOCK_COLUMNS : (hb + 1) * BLOCK_COLUMNS]
+            rows = out_pool.tile([P, TILES * H_BLOCK], F32, name="out_rows")
+            rows_view = rows[:].rearrange("p (h a w e) -> p h a w e", h=2, a=2, e=PAIR)
+            for half in range(TILES // 2):
+                bank = t_psum.tile([P, 2, PAIR, P], F32, name="bank", tag="t")
+                for a in range(2):
+                    for e in range(PAIR):
+                        first = e * NODE_BLOCK + (2 * half + a) * P
+                        nc.tensor.transpose(bank[:, a, e, :], total[:, first : first + P], ident[:])
+                nc.scalar.copy(out=rows_view[:, half], in_=bank[:].rearrange("p a e w -> p a w e"))
+            nc.sync.dma_start(
+                out=out_view[b, :, :, H_BLOCK * hb : H_BLOCK * (hb + 1)],
+                in_=rows[:].rearrange("p (t h) -> p t h", t=TILES),
+            )
+
+        ident = const.tile([P, P], F32)
+        make_identity(nc, ident[:])
+
+        bias_rows = const.tile([P, P], F32)
+        nc.vector.memset(bias_rows[:], 0.0)
+        bias_rows_bf = bias_rows[:].bitcast(BF16)
+        nc.scalar.dma_start(out=bias_rows_bf[0:H_BLOCKS, :], in_=bWf.rearrange("(r c) -> r c", c=H_BLOCK))
+        nc.scalar.dma_start(out=bias_rows_bf[H_BLOCKS : 2 * H_BLOCKS, :], in_=bUf.rearrange("(r c) -> r c", c=H_BLOCK))
+
+        u_raw = {0: load_weight_part(Uf, "u", 0)}
+        w_raw = {0: load_weight_part(Wf, "w", 0)}
+        h_rows = {0: load_children(0)}
+        x_rows = {0: load_x(0)}
+        h_rows[1] = load_children(1)
+        u_raw[1] = load_weight_part(Uf, "u", 1)
+        w_raw[1] = load_weight_part(Wf, "w", 1)
+        c_rows = {0: load_cells(0)}
+        h_rows[2] = load_children(2)
+        c_rows[1] = load_cells(1)
+        c_rows[2] = load_cells(2)
+        x_rows[1] = load_x(1)
+
+        u_codes = weights.tile([P, HIDDEN], U32, align_bytes=64)
+        u_scales = weights.tile([P, HIDDEN], U8, align_bytes=64)
+        w_codes = weights.tile([P, HIDDEN], U32, align_bytes=64)
+        w_scales = weights.tile([P, HIDDEN], U8, align_bytes=64)
+        for hb in range(0, H_BLOCKS // W_PARTS):
+            quantise_weight_blocks(hb)
+
+        bias_ps = t_psum.tile([P, P], F32, name="bias_ps", tag="t")
+        nc.tensor.transpose(bias_ps[:], bias_rows[:], ident[:])
+        both = const.tile([P, 2 * PAIR * H_BLOCKS], F32)
+        nc.vector.tensor_copy(out=both[:], in_=bias_ps[:, 0 : 2 * H_BLOCKS].bitcast(BF16))
+        bias = const.tile([P, PAIR * H_BLOCKS], F32)
+        nc.vector.tensor_tensor(
+            out=bias[:], in0=both[:, 0 : PAIR * H_BLOCKS], in1=both[:, PAIR * H_BLOCKS : 2 * PAIR * H_BLOCKS], op=ADD
+        )
+
+        children = {0: quantise_rows(regroup_rows(transpose_rows(h_rows[0])), "child")}
+        nodes = {0: quantise_rows(regroup_rows(transpose_rows(x_rows[0])), "node")}
+        grouped_1 = regroup_rows(transpose_rows(h_rows[1]))
+        for hb in range(H_BLOCKS // W_PARTS, H_BLOCKS):
+            quantise_weight_blocks(hb)
+        children[1] = quantise_rows(grouped_1, "child")
+        sums = {}
+
+        for s in range(STEPS):
+            b, k = divmod(s, CHILDREN)
+            if s + AHEAD < STEPS:
+                h_rows[s + AHEAD] = load_children(s + AHEAD)
+                c_rows[s + AHEAD] = load_cells(s + AHEAD)
+            gates = {}
+            cells = {}
+            grouped = {}
+            for first_hb in range(0, H_BLOCKS, 2):
+                pair = (first_hb, first_hb + 1)
+                rows_to_prepare = None
+                if first_hb == 0 and k == X_STEP and b + 1 < BLOCKS:
+                    rows_to_prepare = x_rows[b + 1]
+                if first_hb == 2 and s + LEAD < STEPS:
+                    rows_to_prepare = h_rows[s + LEAD]
+
+                z = {}
+                for hb in pair:
+                    for e in range(PAIR):
+                        z[(hb, e)] = gate_sums(hb, e, children[s], nodes[b])
+                if rows_to_prepare is not None:
+                    banks = transpose_rows(rows_to_prepare)
+                for hb in pair:
+                    cells[hb] = transpose_cells(c_rows[s], hb)
+
+                for hb in pair:
+                    gate = gate_pool.tile([P, BLOCK_COLUMNS], F32)
+                    for e in range(PAIR):
+                        nc.scalar.activation(
+                            out=gate[:, e * NODE_BLOCK : (e + 1) * NODE_BLOCK],
+                            in_=z[(hb, e)][:],
+                            func=SIGMOID,
+                            bias=bias[:, PAIR * hb + e : PAIR * hb + e + 1],
+                            scale=1.0,
+                        )
+                    gates[hb] = gate
+                if rows_to_prepare is not None:
+                    grouped[first_hb] = regroup_rows(banks)
+
+                if b > 0 and 1 <= k <= H_BLOCKS // 2:
+                    store_block(b - 1, 2 * (k - 1) + first_hb // 2)
+
+            if k == 0:
+                sums[b] = sum_pool.tile([P, STEP_COLUMNS], F32, name="total")
+                products = sums[b]
+            else:
+                products = prod_pool.tile([P, STEP_COLUMNS], F32, name="products")
+            total = sums[b]
+            for hb in range(H_BLOCKS):
+                first, last = hb * BLOCK_COLUMNS, (hb + 1) * BLOCK_COLUMNS
+                nc.vector.tensor_tensor(
+                    out=products[:, first:last].rearrange("p (e n) -> p e n", e=PAIR),
+                    in0=gates[hb][:].rearrange("p (e n) -> p e n", e=PAIR),
+                    in1=cells[hb][:].bitcast(BF16).rearrange("p (n e) -> p e n", e=PAIR),
+                    op=MULT,
+                )
+                last = min(last, GPSIMD_COLUMNS)
+                if k > 0 and first < last:
+                    nc.gpsimd.tensor_tensor(
+                        out=total[:, first:last], in0=total[:, first:last], in1=products[:, first:last], op=ADD
+                    )
+            if 0 in grouped:
+                nodes[b + 1] = quantise_rows(grouped[0], "node")
+            if 2 in grouped:
+                children[s + LEAD] = quantise_rows(grouped[2], "child")
+            if k == CHILDREN - 1:
+                bounds = [max(hb * BLOCK_COLUMNS, GPSIMD_COLUMNS) for hb in range(H_BLOCKS)] + [STEP_COLUMNS]
+            else:
+                bounds = [GPSIMD_COLUMNS, STEP_COLUMNS]
+            for first, last in zip(bounds[:-1], bounds[1:]):
+                if k > 0 and first < last:
+                    nc.vector.tensor_tensor(
+                        out=total[:, first:last], in0=total[:, first:last], in1=products[:, first:last], op=ADD
+                    )
+
+        for hb in range(H_BLOCKS):
+            store_block(BLOCKS - 1, hb)

@@ -27,6 +27,7 @@ H_BLOCK = PAIR * P
 H_BLOCKS = HIDDEN // H_BLOCK
 W_PARTS = 2
 W_PART = HIDDEN // W_PARTS
+PSUM_BANKS = 8
 STEPS = BLOCKS * CHILDREN
 AHEAD = 3
 LEAD = 2
@@ -52,13 +53,11 @@ def tile_childsumtreelstmcell_pa_t_kernel(tc, x, child_h, child_c, Wf, bWf, Uf, 
         c_rows_pool = ctx.enter_context(tc.tile_pool(name="c_rows", bufs=AHEAD + 1))
         grouped_pool = ctx.enter_context(tc.tile_pool(name="grouped", bufs=3))
         codes_pool = ctx.enter_context(tc.tile_pool(name="codes", bufs=LEAD + 1))
-        gate_pool = ctx.enter_context(tc.tile_pool(name="gate", bufs=6))
+        gate_pool = ctx.enter_context(tc.tile_pool(name="gate", bufs=8))
         prod_pool = ctx.enter_context(tc.tile_pool(name="prod", bufs=2))
         sum_pool = ctx.enter_context(tc.tile_pool(name="sums", bufs=2))
         out_pool = ctx.enter_context(tc.tile_pool(name="out_rows", bufs=H_BLOCKS))
-        z_psum = ctx.enter_context(tc.psum_pool(name="z_psum", bufs=3))
-        c_psum = ctx.enter_context(tc.psum_pool(name="c_psum", bufs=3))
-        t_psum = ctx.enter_context(tc.psum_pool(name="t_psum", bufs=2))
+        banks_pool = ctx.enter_context(tc.psum_pool(name="banks", bufs=PSUM_BANKS))
         ctx.enter_context(tc.manual_schedule())
 
         def load_weight_part(w, name, part):
@@ -108,7 +107,7 @@ def tile_childsumtreelstmcell_pa_t_kernel(tc, x, child_h, child_c, Wf, bWf, Uf, 
             words = rows[:].bitcast(F32)
             banks = []
             for half in range(TILES // 2):
-                bank = t_psum.tile([P, 2, HALVES, P], F32, name="bank", tag="t")
+                bank = banks_pool.tile([P, 2, HALVES, P], F32, name="bank", tag="bank")
                 for a in range(2):
                     for u in range(HALVES):
                         first = (2 * half + a) * WORDS
@@ -130,7 +129,7 @@ def tile_childsumtreelstmcell_pa_t_kernel(tc, x, child_h, child_c, Wf, bWf, Uf, 
             return codes, scales
 
         def gate_sums(hb, e, child, node):
-            z = z_psum.tile([P, NODE_BLOCK], F32)
+            z = banks_pool.tile([P, NODE_BLOCK], F32, name="z", tag="bank")
             cols = slice((PAIR * hb + e) * P, (PAIR * hb + e + 1) * P)
             nc.tensor.matmul_mx(
                 out=z[:],
@@ -154,7 +153,7 @@ def tile_childsumtreelstmcell_pa_t_kernel(tc, x, child_h, child_c, Wf, bWf, Uf, 
 
         def transpose_cells(rows, hb):
             words = rows[:].bitcast(F32)
-            cells = c_psum.tile([P, NODE_BLOCK], F32)
+            cells = banks_pool.tile([P, NODE_BLOCK], F32, name="cells", tag="bank")
             for t in range(TILES):
                 first = t * (HIDDEN // PAIR) + hb * P
                 nc.tensor.transpose(cells[:, t * P : (t + 1) * P], words[:, first : first + P], ident[:])
@@ -165,7 +164,7 @@ def tile_childsumtreelstmcell_pa_t_kernel(tc, x, child_h, child_c, Wf, bWf, Uf, 
             rows = out_pool.tile([P, TILES * H_BLOCK], F32, name="out_rows")
             rows_view = rows[:].rearrange("p (h a w e) -> p h a w e", h=2, a=2, e=PAIR)
             for half in range(TILES // 2):
-                bank = t_psum.tile([P, 2, PAIR, P], F32, name="bank", tag="t")
+                bank = banks_pool.tile([P, 2, PAIR, P], F32, name="bank", tag="bank")
                 for a in range(2):
                     for e in range(PAIR):
                         first = e * NODE_BLOCK + (2 * half + a) * P
@@ -205,7 +204,7 @@ def tile_childsumtreelstmcell_pa_t_kernel(tc, x, child_h, child_c, Wf, bWf, Uf, 
         for hb in range(0, H_BLOCKS // W_PARTS):
             quantise_weight_blocks(hb)
 
-        bias_ps = t_psum.tile([P, P], F32, name="bias_ps", tag="t")
+        bias_ps = banks_pool.tile([P, P], F32, name="bias_ps", tag="bank")
         nc.tensor.transpose(bias_ps[:], bias_rows[:], ident[:])
         both = const.tile([P, 2 * PAIR * H_BLOCKS], F32)
         nc.vector.tensor_copy(out=both[:], in_=bias_ps[:, 0 : 2 * H_BLOCKS].bitcast(BF16))
@@ -230,24 +229,21 @@ def tile_childsumtreelstmcell_pa_t_kernel(tc, x, child_h, child_c, Wf, bWf, Uf, 
             gates = {}
             cells = {}
             grouped = {}
-            for first_hb in range(0, H_BLOCKS, 2):
-                pair = (first_hb, first_hb + 1)
-                rows_to_prepare = None
-                if first_hb == 0 and k == X_STEP and b + 1 < BLOCKS:
-                    rows_to_prepare = x_rows[b + 1]
-                if first_hb == 2 and s + LEAD < STEPS:
-                    rows_to_prepare = h_rows[s + LEAD]
+            run_blocks = H_BLOCKS if s + 1 < STEPS else H_BLOCKS // 2
+            for first_hb in range(0, H_BLOCKS, run_blocks):
+                run = range(first_hb, first_hb + run_blocks)
 
                 z = {}
-                for hb in pair:
+                for hb in run:
                     for e in range(PAIR):
                         z[(hb, e)] = gate_sums(hb, e, children[s], nodes[b])
-                if rows_to_prepare is not None:
-                    banks = transpose_rows(rows_to_prepare)
-                for hb in pair:
+                for hb in run:
                     cells[hb] = transpose_cells(c_rows[s], hb)
+                banks = {}
+                if s + LEAD < STEPS:
+                    banks["child"] = transpose_rows(h_rows[s + LEAD])
 
-                for hb in pair:
+                for hb in run:
                     gate = gate_pool.tile([P, BLOCK_COLUMNS], F32)
                     for e in range(PAIR):
                         nc.scalar.activation(
@@ -258,11 +254,15 @@ def tile_childsumtreelstmcell_pa_t_kernel(tc, x, child_h, child_c, Wf, bWf, Uf, 
                             scale=1.0,
                         )
                     gates[hb] = gate
-                if rows_to_prepare is not None:
-                    grouped[first_hb] = regroup_rows(banks)
+                if "child" in banks:
+                    grouped["child"] = regroup_rows(banks["child"])
 
-                if b > 0 and 1 <= k <= H_BLOCKS // 2:
-                    store_block(b - 1, 2 * (k - 1) + first_hb // 2)
+            if k == X_STEP and b + 1 < BLOCKS:
+                grouped["node"] = regroup_rows(transpose_rows(x_rows[b + 1]))
+
+            if b > 0 and 1 <= k <= H_BLOCKS // 2:
+                for hb in (2 * (k - 1), 2 * (k - 1) + 1):
+                    store_block(b - 1, hb)
 
             if k == 0:
                 sums[b] = sum_pool.tile([P, STEP_COLUMNS], F32, name="total")
@@ -283,10 +283,10 @@ def tile_childsumtreelstmcell_pa_t_kernel(tc, x, child_h, child_c, Wf, bWf, Uf, 
                     nc.gpsimd.tensor_tensor(
                         out=total[:, first:last], in0=total[:, first:last], in1=products[:, first:last], op=ADD
                     )
-            if 0 in grouped:
-                nodes[b + 1] = quantise_rows(grouped[0], "node")
-            if 2 in grouped:
-                children[s + LEAD] = quantise_rows(grouped[2], "child")
+            if "node" in grouped:
+                nodes[b + 1] = quantise_rows(grouped["node"], "node")
+            if "child" in grouped:
+                children[s + LEAD] = quantise_rows(grouped["child"], "child")
             if k == CHILDREN - 1:
                 bounds = [max(hb * BLOCK_COLUMNS, GPSIMD_COLUMNS) for hb in range(H_BLOCKS)] + [STEP_COLUMNS]
             else:

@@ -25,8 +25,7 @@ WORDS = FEATURES // PAIR
 HALVES = WORDS // P
 H_BLOCK = PAIR * P
 H_BLOCKS = HIDDEN // H_BLOCK
-W_PARTS = 2
-W_PART = HIDDEN // W_PARTS
+W_BOUNDS = (0, H_BLOCK, HIDDEN)
 PSUM_BANKS = 8
 STEPS = BLOCKS * CHILDREN
 AHEAD = 3
@@ -34,7 +33,6 @@ LEAD = 2
 X_STEP = 2
 BLOCK_COLUMNS = PAIR * NODE_BLOCK
 STEP_COLUMNS = H_BLOCKS * BLOCK_COLUMNS
-GPSIMD_COLUMNS = BLOCK_COLUMNS
 
 
 def tile_childsumtreelstmcell_pa_t_kernel(tc, x, child_h, child_c, Wf, bWf, Uf, bUf, out):
@@ -47,29 +45,32 @@ def tile_childsumtreelstmcell_pa_t_kernel(tc, x, child_h, child_c, Wf, bWf, Uf, 
     with ExitStack() as ctx:
         const = ctx.enter_context(tc.tile_pool(name="const", bufs=1))
         weights = ctx.enter_context(tc.tile_pool(name="weights", bufs=1))
-        wstage = ctx.enter_context(tc.tile_pool(name="wstage", bufs=2))
+        wstage = ctx.enter_context(tc.tile_pool(name="wstage", bufs=4))
         x_rows_pool = ctx.enter_context(tc.tile_pool(name="x_rows", bufs=BLOCKS))
         h_rows_pool = ctx.enter_context(tc.tile_pool(name="h_rows", bufs=AHEAD))
         c_rows_pool = ctx.enter_context(tc.tile_pool(name="c_rows", bufs=AHEAD + 1))
         grouped_pool = ctx.enter_context(tc.tile_pool(name="grouped", bufs=3))
         codes_pool = ctx.enter_context(tc.tile_pool(name="codes", bufs=LEAD + 1))
-        gate_pool = ctx.enter_context(tc.tile_pool(name="gate", bufs=8))
-        prod_pool = ctx.enter_context(tc.tile_pool(name="prod", bufs=2))
+        gate_pool = ctx.enter_context(tc.tile_pool(name="gate", bufs=6))
+        prod_pool = ctx.enter_context(tc.tile_pool(name="prod", bufs=4))
         sum_pool = ctx.enter_context(tc.tile_pool(name="sums", bufs=2))
-        out_pool = ctx.enter_context(tc.tile_pool(name="out_rows", bufs=H_BLOCKS))
+        out_pool = ctx.enter_context(tc.tile_pool(name="out_rows", bufs=3))
         banks_pool = ctx.enter_context(tc.psum_pool(name="banks", bufs=PSUM_BANKS))
         ctx.enter_context(tc.manual_schedule())
 
         def load_weight_part(w, name, part):
-            raw = weights.tile([P, PACK * W_PART], BF16, name="raw", tag="raw_%s%d" % (name, part))
+            cols = slice(W_BOUNDS[part], W_BOUNDS[part + 1])
+            pool, tag = (weights, "raw_%s" % name) if part == 0 else (prod_pool, "products")
+            raw = pool.tile([P, PACK * (cols.stop - cols.start)], BF16, name="raw", tag=tag)
             nc.sync.dma_start(
                 out=raw[:].rearrange("q (j c) -> q j c", j=PACK),
-                in_=w[:, W_PART * part : W_PART * (part + 1)].rearrange("(q j) c -> q j c", j=PACK),
+                in_=w[:, cols].rearrange("(q j) c -> q j c", j=PACK),
             )
             return raw
 
         def regroup_weight_block(raw_parts, hb):
-            part, first = divmod(H_BLOCK * hb, W_PART)
+            part = 0 if hb == 0 else 1
+            first = H_BLOCK * hb - W_BOUNDS[part]
             grouped_w = wstage.tile([P, H_BLOCK * PACK], BF16, align_bytes=64)
             nc.vector.tensor_copy(
                 out=grouped_w[:].rearrange("q (e m j) -> q e m j", e=PAIR, j=PACK),
@@ -79,12 +80,9 @@ def tile_childsumtreelstmcell_pa_t_kernel(tc, x, child_h, child_c, Wf, bWf, Uf, 
             )
             return grouped_w
 
-        def quantise_weight_blocks(hb):
+        def quantise_weight_block(grouped_w, codes, scales, hb):
             cols = slice(H_BLOCK * hb, H_BLOCK * (hb + 1))
-            grouped_u = regroup_weight_block(u_raw, hb)
-            grouped_w = regroup_weight_block(w_raw, hb)
-            nc.vector.quantize_mx(out=u_codes[:, cols].bitcast(FP8X4), scales=u_scales[:, cols], in_=grouped_u[:])
-            nc.vector.quantize_mx(out=w_codes[:, cols].bitcast(FP8X4), scales=w_scales[:, cols], in_=grouped_w[:])
+            nc.vector.quantize_mx(out=codes[:, cols].bitcast(FP8X4), scales=scales[:, cols], in_=grouped_w[:])
 
         def load_x(b):
             rows = x_rows_pool.tile([P, TILES * FEATURES], BF16, name="x_rows")
@@ -159,24 +157,49 @@ def tile_childsumtreelstmcell_pa_t_kernel(tc, x, child_h, child_c, Wf, bWf, Uf, 
                 nc.tensor.transpose(cells[:, t * P : (t + 1) * P], words[:, first : first + P], ident[:])
             return cells
 
-        def store_block(b, hb):
-            total = sums[b][:, hb * BLOCK_COLUMNS : (hb + 1) * BLOCK_COLUMNS]
+        def block_columns(hb, count=1):
+            return slice(hb * BLOCK_COLUMNS, (hb + count) * BLOCK_COLUMNS)
+
+        def add(engine, into, other, cols):
+            engine.tensor_tensor(out=into[:, cols], in0=into[:, cols], in1=other[:, cols], op=ADD)
+
+        def store_block(b, hb, tiles, finish=False):
+            terms = [tile[:, block_columns(hb)] for tile in tiles]
             rows = out_pool.tile([P, TILES * H_BLOCK], F32, name="out_rows")
             rows_view = rows[:].rearrange("p (h a w e) -> p h a w e", h=2, a=2, e=PAIR)
+            out_rows = rows[:].rearrange("p (t h) -> p t h", t=TILES)
+            out_cols = slice(H_BLOCK * hb, H_BLOCK * (hb + 1))
             for half in range(TILES // 2):
                 bank = banks_pool.tile([P, 2, PAIR, P], F32, name="bank", tag="bank")
                 for a in range(2):
                     for e in range(PAIR):
                         first = e * NODE_BLOCK + (2 * half + a) * P
-                        nc.tensor.transpose(bank[:, a, e, :], total[:, first : first + P], ident[:])
-                nc.scalar.copy(out=rows_view[:, half], in_=bank[:].rearrange("p a e w -> p a w e"))
-            nc.sync.dma_start(
-                out=out_view[b, :, :, H_BLOCK * hb : H_BLOCK * (hb + 1)],
-                in_=rows[:].rearrange("p (t h) -> p t h", t=TILES),
-            )
+                        for i, term in enumerate(terms):
+                            nc.tensor.matmul(
+                                bank[:, a, e, :],
+                                lhsT=term[:, first : first + P],
+                                rhs=ident[:],
+                                start=i == 0,
+                                stop=i == len(terms) - 1,
+                                is_transpose=True,
+                            )
+                bank_view = bank[:].rearrange("p a e w -> p a w e")
+                if finish and half == 1:
+                    nc.vector.tensor_copy(out=rows_view[:, half], in_=bank_view)
+                else:
+                    nc.scalar.copy(out=rows_view[:, half], in_=bank_view)
+                if finish:
+                    two = slice(2 * half, 2 * half + 2)
+                    nc.sync.dma_start(out=out_view[b, :, two, out_cols], in_=out_rows[:, two, :])
+            if not finish:
+                nc.sync.dma_start(out=out_view[b, :, :, out_cols], in_=out_rows)
 
         ident = const.tile([P, P], F32)
         make_identity(nc, ident[:])
+
+        first_sigmoid = const.tile([P, 1], F32)
+        nc.gpsimd.memset(first_sigmoid[:], 0.0)
+        nc.scalar.activation(out=first_sigmoid[:], in_=first_sigmoid[:], func=SIGMOID)
 
         bias_rows = const.tile([P, P], F32)
         nc.vector.memset(bias_rows[:], 0.0)
@@ -185,12 +208,12 @@ def tile_childsumtreelstmcell_pa_t_kernel(tc, x, child_h, child_c, Wf, bWf, Uf, 
         nc.scalar.dma_start(out=bias_rows_bf[H_BLOCKS : 2 * H_BLOCKS, :], in_=bUf.rearrange("(r c) -> r c", c=H_BLOCK))
 
         u_raw = {0: load_weight_part(Uf, "u", 0)}
-        w_raw = {0: load_weight_part(Wf, "w", 0)}
         h_rows = {0: load_children(0)}
+        w_raw = {0: load_weight_part(Wf, "w", 0)}
         x_rows = {0: load_x(0)}
-        h_rows[1] = load_children(1)
         u_raw[1] = load_weight_part(Uf, "u", 1)
         w_raw[1] = load_weight_part(Wf, "w", 1)
+        h_rows[1] = load_children(1)
         c_rows = {0: load_cells(0)}
         h_rows[2] = load_children(2)
         c_rows[1] = load_cells(1)
@@ -201,8 +224,16 @@ def tile_childsumtreelstmcell_pa_t_kernel(tc, x, child_h, child_c, Wf, bWf, Uf, 
         u_scales = weights.tile([P, HIDDEN], U8, align_bytes=64)
         w_codes = weights.tile([P, HIDDEN], U32, align_bytes=64)
         w_scales = weights.tile([P, HIDDEN], U8, align_bytes=64)
-        for hb in range(0, H_BLOCKS // W_PARTS):
-            quantise_weight_blocks(hb)
+        h_banks = transpose_rows(h_rows[0])
+        x_banks = transpose_rows(x_rows[0])
+        h_grouped = regroup_rows(h_banks)
+        x_grouped = regroup_rows(x_banks)
+        grouped_u = regroup_weight_block(u_raw, 0)
+        grouped_w = regroup_weight_block(w_raw, 0)
+        children = {0: quantise_rows(h_grouped, "child")}
+        quantise_weight_block(grouped_u, u_codes, u_scales, 0)
+        quantise_weight_block(grouped_w, w_codes, w_scales, 0)
+        nodes = {0: quantise_rows(x_grouped, "node")}
 
         bias_ps = banks_pool.tile([P, P], F32, name="bias_ps", tag="bank")
         nc.tensor.transpose(bias_ps[:], bias_rows[:], ident[:])
@@ -212,14 +243,9 @@ def tile_childsumtreelstmcell_pa_t_kernel(tc, x, child_h, child_c, Wf, bWf, Uf, 
         nc.vector.tensor_tensor(
             out=bias[:], in0=both[:, 0 : PAIR * H_BLOCKS], in1=both[:, PAIR * H_BLOCKS : 2 * PAIR * H_BLOCKS], op=ADD
         )
-
-        children = {0: quantise_rows(regroup_rows(transpose_rows(h_rows[0])), "child")}
-        nodes = {0: quantise_rows(regroup_rows(transpose_rows(x_rows[0])), "node")}
-        grouped_1 = regroup_rows(transpose_rows(h_rows[1]))
-        for hb in range(H_BLOCKS // W_PARTS, H_BLOCKS):
-            quantise_weight_blocks(hb)
-        children[1] = quantise_rows(grouped_1, "child")
         sums = {}
+        products = {}
+        pair_ends = [s for s in range(1, STEPS - CHILDREN, 2)] + [s for s in range(STEPS - CHILDREN + 2, STEPS - 2, 2)]
 
         for s in range(STEPS):
             b, k = divmod(s, CHILDREN)
@@ -229,19 +255,32 @@ def tile_childsumtreelstmcell_pa_t_kernel(tc, x, child_h, child_c, Wf, bWf, Uf, 
             gates = {}
             cells = {}
             grouped = {}
-            run_blocks = H_BLOCKS if s + 1 < STEPS else H_BLOCKS // 2
+            run_blocks = {0: 1, STEPS - 1: H_BLOCKS // 2}.get(s, H_BLOCKS)
             for first_hb in range(0, H_BLOCKS, run_blocks):
                 run = range(first_hb, first_hb + run_blocks)
+                if s == 0 and first_hb > 0:
+                    grouped_u = regroup_weight_block(u_raw, first_hb)
+                    grouped_w = regroup_weight_block(w_raw, first_hb)
+                    quantise_weight_block(grouped_u, u_codes, u_scales, first_hb)
+                    quantise_weight_block(grouped_w, w_codes, w_scales, first_hb)
 
+                if s == STEPS - 1:
+                    for hb in run:
+                        cells[hb] = transpose_cells(c_rows[s], hb)
                 z = {}
                 for hb in run:
                     for e in range(PAIR):
                         z[(hb, e)] = gate_sums(hb, e, children[s], nodes[b])
-                for hb in run:
-                    cells[hb] = transpose_cells(c_rows[s], hb)
-                banks = {}
-                if s + LEAD < STEPS:
-                    banks["child"] = transpose_rows(h_rows[s + LEAD])
+                if s < STEPS - 1:
+                    for hb in run:
+                        cells[hb] = transpose_cells(c_rows[s], hb)
+                rows_to_prepare = None
+                if s == 0 and first_hb == 1:
+                    rows_to_prepare = 1
+                if run[-1] == H_BLOCKS - 1 and s + LEAD < STEPS:
+                    rows_to_prepare = s + LEAD
+                if rows_to_prepare is not None:
+                    banks = transpose_rows(h_rows[rows_to_prepare])
 
                 for hb in run:
                     gate = gate_pool.tile([P, BLOCK_COLUMNS], F32)
@@ -254,48 +293,46 @@ def tile_childsumtreelstmcell_pa_t_kernel(tc, x, child_h, child_c, Wf, bWf, Uf, 
                             scale=1.0,
                         )
                     gates[hb] = gate
-                if "child" in banks:
-                    grouped["child"] = regroup_rows(banks["child"])
+                if rows_to_prepare is not None:
+                    grouped[rows_to_prepare] = regroup_rows(banks)
+                if s == 0 and first_hb == 2:
+                    children[1] = quantise_rows(grouped[1], "child")
 
             if k == X_STEP and b + 1 < BLOCKS:
                 grouped["node"] = regroup_rows(transpose_rows(x_rows[b + 1]))
 
             if b > 0 and 1 <= k <= H_BLOCKS // 2:
                 for hb in (2 * (k - 1), 2 * (k - 1) + 1):
-                    store_block(b - 1, hb)
+                    store_block(b - 1, hb, [sums[b - 1]])
 
             if k == 0:
-                sums[b] = sum_pool.tile([P, STEP_COLUMNS], F32, name="total")
-                products = sums[b]
+                products[s] = sum_pool.tile([P, STEP_COLUMNS], F32, name="total")
+                sums[b] = products[s]
             else:
-                products = prod_pool.tile([P, STEP_COLUMNS], F32, name="products")
-            total = sums[b]
+                products[s] = prod_pool.tile([P, STEP_COLUMNS], F32, name="products")
             for hb in range(H_BLOCKS):
-                first, last = hb * BLOCK_COLUMNS, (hb + 1) * BLOCK_COLUMNS
+                if s == STEPS - 1:
+                    add(nc.vector, products[s - 2], products[s - 1], block_columns(hb))
                 nc.vector.tensor_tensor(
-                    out=products[:, first:last].rearrange("p (e n) -> p e n", e=PAIR),
+                    out=products[s][:, block_columns(hb)].rearrange("p (e n) -> p e n", e=PAIR),
                     in0=gates[hb][:].rearrange("p (e n) -> p e n", e=PAIR),
                     in1=cells[hb][:].bitcast(BF16).rearrange("p (n e) -> p e n", e=PAIR),
                     op=MULT,
                 )
-                last = min(last, GPSIMD_COLUMNS)
-                if k > 0 and first < last:
-                    nc.gpsimd.tensor_tensor(
-                        out=total[:, first:last], in0=total[:, first:last], in1=products[:, first:last], op=ADD
-                    )
             if "node" in grouped:
                 nodes[b + 1] = quantise_rows(grouped["node"], "node")
-            if "child" in grouped:
-                children[s + LEAD] = quantise_rows(grouped["child"], "child")
-            if k == CHILDREN - 1:
-                bounds = [max(hb * BLOCK_COLUMNS, GPSIMD_COLUMNS) for hb in range(H_BLOCKS)] + [STEP_COLUMNS]
-            else:
-                bounds = [GPSIMD_COLUMNS, STEP_COLUMNS]
-            for first, last in zip(bounds[:-1], bounds[1:]):
-                if k > 0 and first < last:
-                    nc.vector.tensor_tensor(
-                        out=total[:, first:last], in0=total[:, first:last], in1=products[:, first:last], op=ADD
-                    )
+            if s + LEAD < STEPS:
+                children[s + LEAD] = quantise_rows(grouped[s + LEAD], "child")
+            for second, first_hb in ((s, 0), (s - 1, H_BLOCKS // 2)):
+                if second in pair_ends:
+                    total = sums[second // CHILDREN]
+                    pair_sum = products[second - 1]
+                    add(nc.vector, pair_sum, products[second], block_columns(first_hb, H_BLOCKS // 2))
+                    if pair_sum is not total:
+                        for hb in range(first_hb, first_hb + H_BLOCKS // 2):
+                            add(nc.gpsimd, total, pair_sum, block_columns(hb))
 
         for hb in range(H_BLOCKS):
-            store_block(BLOCKS - 1, hb)
+            store_block(
+                BLOCKS - 1, hb, [sums[BLOCKS - 1], products[STEPS - 3], products[STEPS - 1]], finish=hb == H_BLOCKS - 1
+            )

@@ -25,14 +25,16 @@ WORDS = FEATURES // PAIR
 HALVES = WORDS // P
 H_BLOCK = PAIR * P
 H_BLOCKS = HIDDEN // H_BLOCK
-W_BOUNDS = (0, H_BLOCK, HIDDEN)
+W_BOUNDS = (0, H_BLOCK, 2 * H_BLOCK, HIDDEN)
 PSUM_BANKS = 8
+TWO = 2
+RUNS_PER_PAIR = H_BLOCKS // TWO
+RUNS_PER_BLOCK = CHILDREN // TWO * RUNS_PER_PAIR
+RUNS = BLOCKS * RUNS_PER_BLOCK
 STEPS = BLOCKS * CHILDREN
-AHEAD = 3
-LEAD = 2
-X_STEP = 2
 BLOCK_COLUMNS = PAIR * NODE_BLOCK
-STEP_COLUMNS = H_BLOCKS * BLOCK_COLUMNS
+RUN_COLUMNS = TWO * BLOCK_COLUMNS
+X_RUN = 3
 
 
 def tile_childsumtreelstmcell_pa_t_kernel(tc, x, child_h, child_c, Wf, bWf, Uf, bUf, out):
@@ -47,20 +49,22 @@ def tile_childsumtreelstmcell_pa_t_kernel(tc, x, child_h, child_c, Wf, bWf, Uf, 
         weights = ctx.enter_context(tc.tile_pool(name="weights", bufs=1))
         wstage = ctx.enter_context(tc.tile_pool(name="wstage", bufs=4))
         x_rows_pool = ctx.enter_context(tc.tile_pool(name="x_rows", bufs=BLOCKS))
-        h_rows_pool = ctx.enter_context(tc.tile_pool(name="h_rows", bufs=AHEAD))
-        c_rows_pool = ctx.enter_context(tc.tile_pool(name="c_rows", bufs=AHEAD + 1))
+        h_rows_pool = ctx.enter_context(tc.tile_pool(name="h_rows", bufs=4))
+        c_rows_pool = ctx.enter_context(tc.tile_pool(name="c_rows", bufs=8))
         grouped_pool = ctx.enter_context(tc.tile_pool(name="grouped", bufs=3))
-        codes_pool = ctx.enter_context(tc.tile_pool(name="codes", bufs=LEAD + 1))
+        child_codes_pool = ctx.enter_context(tc.tile_pool(name="child_codes", bufs=5))
+        node_codes_pool = ctx.enter_context(tc.tile_pool(name="node_codes", bufs=BLOCKS))
         gate_pool = ctx.enter_context(tc.tile_pool(name="gate", bufs=6))
-        prod_pool = ctx.enter_context(tc.tile_pool(name="prod", bufs=4))
-        sum_pool = ctx.enter_context(tc.tile_pool(name="sums", bufs=2))
+        prod_pool = ctx.enter_context(tc.tile_pool(name="prod", bufs=3))
+        sum_pool = ctx.enter_context(tc.tile_pool(name="sums", bufs=BLOCKS))
         out_pool = ctx.enter_context(tc.tile_pool(name="out_rows", bufs=3))
         banks_pool = ctx.enter_context(tc.psum_pool(name="banks", bufs=PSUM_BANKS))
         ctx.enter_context(tc.manual_schedule())
 
         def load_weight_part(w, name, part):
             cols = slice(W_BOUNDS[part], W_BOUNDS[part + 1])
-            pool, tag = (weights, "raw_%s" % name) if part == 0 else (prod_pool, "products")
+            last = part == len(W_BOUNDS) - 2
+            pool, tag = (prod_pool, "products") if last else (weights, "raw_%s%d" % (name, part))
             raw = pool.tile([P, PACK * (cols.stop - cols.start)], BF16, name="raw", tag=tag)
             nc.sync.dma_start(
                 out=raw[:].rearrange("q (j c) -> q j c", j=PACK),
@@ -69,7 +73,7 @@ def tile_childsumtreelstmcell_pa_t_kernel(tc, x, child_h, child_c, Wf, bWf, Uf, 
             return raw
 
         def regroup_weight_block(raw_parts, hb):
-            part = 0 if hb == 0 else 1
+            part = min(hb, len(W_BOUNDS) - 2)
             first = H_BLOCK * hb - W_BOUNDS[part]
             grouped_w = wstage.tile([P, H_BLOCK * PACK], BF16, align_bytes=64)
             nc.vector.tensor_copy(
@@ -89,16 +93,23 @@ def tile_childsumtreelstmcell_pa_t_kernel(tc, x, child_h, child_c, Wf, bWf, Uf, 
             nc.sync.dma_start(out=rows[:], in_=x_view[b])
             return rows
 
-        def load_children(s):
+        def load_child(s):
             b, k = divmod(s, CHILDREN)
             rows = h_rows_pool.tile([P, TILES * FEATURES], BF16, name="h_rows")
             nc.sync.dma_start(out=rows[:].rearrange("p (t d) -> p t d", t=TILES), in_=h_view[b, :, :, k, :])
             return rows
 
-        def load_cells(s):
-            b, k = divmod(s, CHILDREN)
-            rows = c_rows_pool.tile([P, TILES * HIDDEN], BF16, name="c_rows")
-            nc.sync.dma_start(out=rows[:].rearrange("p (t h) -> p t h", t=TILES), in_=c_view[b, :, :, k, :])
+        def load_cells(r):
+            pair, half = divmod(r, RUNS_PER_PAIR)
+            rows = []
+            for s in (TWO * pair, TWO * pair + 1):
+                b, k = divmod(s, CHILDREN)
+                cells = c_rows_pool.tile([P, TILES * TWO * H_BLOCK], BF16, name="c_rows")
+                nc.sync.dma_start(
+                    out=cells[:].rearrange("p (t h) -> p t h", t=TILES),
+                    in_=c_view[b, :, :, k, TWO * H_BLOCK * half : TWO * H_BLOCK * (half + 1)],
+                )
+                rows.append(cells)
             return rows
 
         def transpose_rows(rows):
@@ -120,9 +131,9 @@ def tile_childsumtreelstmcell_pa_t_kernel(tc, x, child_h, child_c, Wf, bWf, Uf, 
                 nc.scalar.copy(out=grouped_words[:, half], in_=banks[half][:].rearrange("p a u n -> p a n u"))
             return grouped
 
-        def quantise_rows(grouped, kind):
-            codes = codes_pool.tile([P, NODE_BLOCK], U32, name="codes", tag="%s_codes" % kind, align_bytes=64)
-            scales = codes_pool.tile([P, NODE_BLOCK], U8, name="scales", tag="%s_scales" % kind, align_bytes=64)
+        def quantise_rows(grouped, pool):
+            codes = pool.tile([P, NODE_BLOCK], U32, name="codes", align_bytes=64)
+            scales = pool.tile([P, NODE_BLOCK], U8, name="scales", align_bytes=64)
             nc.vector.quantize_mx(out=codes[:].bitcast(FP8X4), scales=scales[:], in_=grouped[:])
             return codes, scales
 
@@ -149,22 +160,23 @@ def tile_childsumtreelstmcell_pa_t_kernel(tc, x, child_h, child_c, Wf, bWf, Uf, 
             )
             return z
 
-        def transpose_cells(rows, hb):
+        def transpose_cells(rows, j):
             words = rows[:].bitcast(F32)
             cells = banks_pool.tile([P, NODE_BLOCK], F32, name="cells", tag="bank")
             for t in range(TILES):
-                first = t * (HIDDEN // PAIR) + hb * P
+                first = (TWO * t + j) * P
                 nc.tensor.transpose(cells[:, t * P : (t + 1) * P], words[:, first : first + P], ident[:])
             return cells
 
-        def block_columns(hb, count=1):
-            return slice(hb * BLOCK_COLUMNS, (hb + count) * BLOCK_COLUMNS)
+        def multiply(products, unit, gate, cells):
+            nc.vector.tensor_tensor(
+                out=products[:, unit * BLOCK_COLUMNS : (unit + 1) * BLOCK_COLUMNS].rearrange("p (e n) -> p e n", e=PAIR),
+                in0=gate[:].rearrange("p (e n) -> p e n", e=PAIR),
+                in1=cells[:].bitcast(BF16).rearrange("p (n e) -> p e n", e=PAIR),
+                op=MULT,
+            )
 
-        def add(engine, into, other, cols):
-            engine.tensor_tensor(out=into[:, cols], in0=into[:, cols], in1=other[:, cols], op=ADD)
-
-        def store_block(b, hb, tiles, finish=False):
-            terms = [tile[:, block_columns(hb)] for tile in tiles]
+        def store_block(b, hb, terms, split=False):
             rows = out_pool.tile([P, TILES * H_BLOCK], F32, name="out_rows")
             rows_view = rows[:].rearrange("p (h a w e) -> p h a w e", h=2, a=2, e=PAIR)
             out_rows = rows[:].rearrange("p (t h) -> p t h", t=TILES)
@@ -184,39 +196,47 @@ def tile_childsumtreelstmcell_pa_t_kernel(tc, x, child_h, child_c, Wf, bWf, Uf, 
                                 is_transpose=True,
                             )
                 bank_view = bank[:].rearrange("p a e w -> p a w e")
-                if finish and half == 1:
+                if split and half == 1:
                     nc.vector.tensor_copy(out=rows_view[:, half], in_=bank_view)
                 else:
                     nc.scalar.copy(out=rows_view[:, half], in_=bank_view)
-                if finish:
+                if split:
                     two = slice(2 * half, 2 * half + 2)
                     nc.sync.dma_start(out=out_view[b, :, two, out_cols], in_=out_rows[:, two, :])
-            if not finish:
+            if not split:
                 nc.sync.dma_start(out=out_view[b, :, :, out_cols], in_=out_rows)
+
+        def sum_columns(hb):
+            return slice(hb * BLOCK_COLUMNS, (hb + 1) * BLOCK_COLUMNS)
 
         ident = const.tile([P, P], F32)
         make_identity(nc, ident[:])
 
-        first_sigmoid = const.tile([P, 1], F32)
-        nc.gpsimd.memset(first_sigmoid[:], 0.0)
-        nc.scalar.activation(out=first_sigmoid[:], in_=first_sigmoid[:], func=SIGMOID)
-
         bias_rows = const.tile([P, P], F32)
         nc.vector.memset(bias_rows[:], 0.0)
         bias_rows_bf = bias_rows[:].bitcast(BF16)
-        nc.scalar.dma_start(out=bias_rows_bf[0:H_BLOCKS, :], in_=bWf.rearrange("(r c) -> r c", c=H_BLOCK))
-        nc.scalar.dma_start(out=bias_rows_bf[H_BLOCKS : 2 * H_BLOCKS, :], in_=bUf.rearrange("(r c) -> r c", c=H_BLOCK))
+        nc.sync.dma_start(out=bias_rows_bf[0:H_BLOCKS, :], in_=bWf.rearrange("(r c) -> r c", c=H_BLOCK))
+        nc.sync.dma_start(out=bias_rows_bf[H_BLOCKS : 2 * H_BLOCKS, :], in_=bUf.rearrange("(r c) -> r c", c=H_BLOCK))
 
-        u_raw = {0: load_weight_part(Uf, "u", 0)}
-        h_rows = {0: load_children(0)}
-        w_raw = {0: load_weight_part(Wf, "w", 0)}
+        first_sigmoid = const.tile([P, 1], F32)
+        nc.vector.memset(first_sigmoid[:], 0.0)
+        nc.scalar.activation(out=first_sigmoid[:], in_=first_sigmoid[:], func=SIGMOID)
+
+        u_raw = {}
+        w_raw = {}
+        h_rows = {0: load_child(0)}
+        u_raw[0] = load_weight_part(Uf, "u", 0)
         x_rows = {0: load_x(0)}
+        w_raw[0] = load_weight_part(Wf, "w", 0)
+        h_rows[1] = load_child(1)
         u_raw[1] = load_weight_part(Uf, "u", 1)
         w_raw[1] = load_weight_part(Wf, "w", 1)
-        h_rows[1] = load_children(1)
         c_rows = {0: load_cells(0)}
-        h_rows[2] = load_children(2)
+        u_raw[2] = load_weight_part(Uf, "u", 2)
+        w_raw[2] = load_weight_part(Wf, "w", 2)
+        h_rows[2] = load_child(2)
         c_rows[1] = load_cells(1)
+        h_rows[3] = load_child(3)
         c_rows[2] = load_cells(2)
         x_rows[1] = load_x(1)
 
@@ -224,115 +244,120 @@ def tile_childsumtreelstmcell_pa_t_kernel(tc, x, child_h, child_c, Wf, bWf, Uf, 
         u_scales = weights.tile([P, HIDDEN], U8, align_bytes=64)
         w_codes = weights.tile([P, HIDDEN], U32, align_bytes=64)
         w_scales = weights.tile([P, HIDDEN], U8, align_bytes=64)
-        h_banks = transpose_rows(h_rows[0])
-        x_banks = transpose_rows(x_rows[0])
-        h_grouped = regroup_rows(h_banks)
-        x_grouped = regroup_rows(x_banks)
+
+        banks_h0 = transpose_rows(h_rows[0])
+        banks_x0 = transpose_rows(x_rows[0])
+        grouped_h0 = regroup_rows(banks_h0)
+        grouped_x0 = regroup_rows(banks_x0)
         grouped_u = regroup_weight_block(u_raw, 0)
         grouped_w = regroup_weight_block(w_raw, 0)
-        children = {0: quantise_rows(h_grouped, "child")}
+        children = {0: quantise_rows(grouped_h0, child_codes_pool)}
         quantise_weight_block(grouped_u, u_codes, u_scales, 0)
         quantise_weight_block(grouped_w, w_codes, w_scales, 0)
-        nodes = {0: quantise_rows(x_grouped, "node")}
+        nodes = {0: quantise_rows(grouped_x0, node_codes_pool)}
 
         bias_ps = banks_pool.tile([P, P], F32, name="bias_ps", tag="bank")
         nc.tensor.transpose(bias_ps[:], bias_rows[:], ident[:])
+        grouped_h1 = regroup_rows(transpose_rows(h_rows[1]))
         both = const.tile([P, 2 * PAIR * H_BLOCKS], F32)
         nc.vector.tensor_copy(out=both[:], in_=bias_ps[:, 0 : 2 * H_BLOCKS].bitcast(BF16))
         bias = const.tile([P, PAIR * H_BLOCKS], F32)
         nc.vector.tensor_tensor(
             out=bias[:], in0=both[:, 0 : PAIR * H_BLOCKS], in1=both[:, PAIR * H_BLOCKS : 2 * PAIR * H_BLOCKS], op=ADD
         )
+        grouped_u = regroup_weight_block(u_raw, 1)
+        children[1] = quantise_rows(grouped_h1, child_codes_pool)
+        grouped_w = regroup_weight_block(w_raw, 1)
+        quantise_weight_block(grouped_u, u_codes, u_scales, 1)
+        quantise_weight_block(grouped_w, w_codes, w_scales, 1)
         sums = {}
-        products = {}
-        pair_ends = [s for s in range(1, STEPS - CHILDREN, 2)] + [s for s in range(STEPS - CHILDREN + 2, STEPS - 2, 2)]
+        pending = []
 
-        for s in range(STEPS):
-            b, k = divmod(s, CHILDREN)
-            if s + AHEAD < STEPS:
-                h_rows[s + AHEAD] = load_children(s + AHEAD)
-                c_rows[s + AHEAD] = load_cells(s + AHEAD)
-            gates = {}
+        for r in range(RUNS):
+            pair, half = divmod(r, RUNS_PER_PAIR)
+            b = r // RUNS_PER_BLOCK
+            units = [(j, i) for j in range(TWO) for i in range(TWO)]
+            prepare = r + 3
+            also = 2 if r == 0 else None
+            last_run = r == RUNS - 1
+            if r + 4 < STEPS:
+                h_rows[r + 4] = load_child(r + 4)
+            if r + 3 < RUNS:
+                c_rows[r + 3] = load_cells(r + 3)
+
+            z = {}
             cells = {}
+            gates = {}
             grouped = {}
-            run_blocks = {0: 1, STEPS - 1: H_BLOCKS // 2}.get(s, H_BLOCKS)
-            for first_hb in range(0, H_BLOCKS, run_blocks):
-                run = range(first_hb, first_hb + run_blocks)
-                if s == 0 and first_hb > 0:
-                    grouped_u = regroup_weight_block(u_raw, first_hb)
-                    grouped_w = regroup_weight_block(w_raw, first_hb)
-                    quantise_weight_block(grouped_u, u_codes, u_scales, first_hb)
-                    quantise_weight_block(grouped_w, w_codes, w_scales, first_hb)
-
-                if s == STEPS - 1:
-                    for hb in run:
-                        cells[hb] = transpose_cells(c_rows[s], hb)
-                z = {}
-                for hb in run:
+            groups = [units[:2], units[2:]] if last_run else [units]
+            for g, group in enumerate(groups):
+                if last_run:
+                    for j, i in group:
+                        cells[(j, i)] = transpose_cells(c_rows[r][i], j)
+                for j, i in group:
                     for e in range(PAIR):
-                        z[(hb, e)] = gate_sums(hb, e, children[s], nodes[b])
-                if s < STEPS - 1:
-                    for hb in run:
-                        cells[hb] = transpose_cells(c_rows[s], hb)
-                rows_to_prepare = None
-                if s == 0 and first_hb == 1:
-                    rows_to_prepare = 1
-                if run[-1] == H_BLOCKS - 1 and s + LEAD < STEPS:
-                    rows_to_prepare = s + LEAD
-                if rows_to_prepare is not None:
-                    banks = transpose_rows(h_rows[rows_to_prepare])
-
-                for hb in run:
+                        z[(j, i, e)] = gate_sums(TWO * half + j, e, children[TWO * pair + i], nodes[b])
+                if not last_run:
+                    for j, i in group:
+                        cells[(j, i)] = transpose_cells(c_rows[r][i], j)
+                for j, i in group:
                     gate = gate_pool.tile([P, BLOCK_COLUMNS], F32)
                     for e in range(PAIR):
+                        hb = TWO * half + j
                         nc.scalar.activation(
                             out=gate[:, e * NODE_BLOCK : (e + 1) * NODE_BLOCK],
-                            in_=z[(hb, e)][:],
+                            in_=z[(j, i, e)][:],
                             func=SIGMOID,
                             bias=bias[:, PAIR * hb + e : PAIR * hb + e + 1],
                             scale=1.0,
                         )
-                    gates[hb] = gate
-                if rows_to_prepare is not None:
-                    grouped[rows_to_prepare] = regroup_rows(banks)
-                if s == 0 and first_hb == 2:
-                    children[1] = quantise_rows(grouped[1], "child")
+                    gates[(j, i)] = gate
 
-            if k == X_STEP and b + 1 < BLOCKS:
+            for s in (also, prepare):
+                if s is not None and s < STEPS:
+                    grouped[s] = regroup_rows(transpose_rows(h_rows[s]))
+            if r % RUNS_PER_BLOCK == X_RUN and b + 1 < BLOCKS:
                 grouped["node"] = regroup_rows(transpose_rows(x_rows[b + 1]))
 
-            if b > 0 and 1 <= k <= H_BLOCKS // 2:
-                for hb in (2 * (k - 1), 2 * (k - 1) + 1):
-                    store_block(b - 1, hb, [sums[b - 1]])
+            if b > 0 and r % RUNS_PER_BLOCK < RUNS_PER_PAIR:
+                for hb in (TWO * half, TWO * half + 1):
+                    store_block(b - 1, hb, [sums[b - 1][:, sum_columns(hb)]])
 
-            if k == 0:
-                products[s] = sum_pool.tile([P, STEP_COLUMNS], F32, name="total")
-                sums[b] = products[s]
-            else:
-                products[s] = prod_pool.tile([P, STEP_COLUMNS], F32, name="products")
-            for hb in range(H_BLOCKS):
-                if s == STEPS - 1:
-                    add(nc.vector, products[s - 2], products[s - 1], block_columns(hb))
-                nc.vector.tensor_tensor(
-                    out=products[s][:, block_columns(hb)].rearrange("p (e n) -> p e n", e=PAIR),
-                    in0=gates[hb][:].rearrange("p (e n) -> p e n", e=PAIR),
-                    in1=cells[hb][:].bitcast(BF16).rearrange("p (n e) -> p e n", e=PAIR),
-                    op=MULT,
-                )
+            if r == 0:
+                for hb in range(TWO, H_BLOCKS):
+                    grouped_u = regroup_weight_block(u_raw, hb)
+                    grouped_w = regroup_weight_block(w_raw, hb)
+                    quantise_weight_block(grouped_u, u_codes, u_scales, hb)
+                    quantise_weight_block(grouped_w, w_codes, w_scales, hb)
+            if r % RUNS_PER_BLOCK == 0:
+                sums[b] = sum_pool.tile([P, H_BLOCKS * BLOCK_COLUMNS], F32, name="total")
+            products = prod_pool.tile([P, TWO * RUN_COLUMNS], F32, name="products", tag="products")
+            first_child, second_child = products[:, 0:RUN_COLUMNS], products[:, RUN_COLUMNS : 2 * RUN_COLUMNS]
+            total = sums[b][:, half * RUN_COLUMNS : (half + 1) * RUN_COLUMNS]
+            for j, i in units:
+                multiply(products, TWO * i + j, gates[(j, i)], cells[(j, i)])
+                if last_run and i == 0:
+                    cols = slice(j * BLOCK_COLUMNS, (j + 1) * BLOCK_COLUMNS)
+                    nc.gpsimd.tensor_tensor(out=total[:, cols], in0=total[:, cols], in1=first_child[:, cols], op=ADD)
             if "node" in grouped:
-                nodes[b + 1] = quantise_rows(grouped["node"], "node")
-            if s + LEAD < STEPS:
-                children[s + LEAD] = quantise_rows(grouped[s + LEAD], "child")
-            for second, first_hb in ((s, 0), (s - 1, H_BLOCKS // 2)):
-                if second in pair_ends:
-                    total = sums[second // CHILDREN]
-                    pair_sum = products[second - 1]
-                    add(nc.vector, pair_sum, products[second], block_columns(first_hb, H_BLOCKS // 2))
-                    if pair_sum is not total:
-                        for hb in range(first_hb, first_hb + H_BLOCKS // 2):
-                            add(nc.gpsimd, total, pair_sum, block_columns(hb))
+                nodes[b + 1] = quantise_rows(grouped["node"], node_codes_pool)
+            for s in (also, prepare):
+                if s in grouped:
+                    children[s] = quantise_rows(grouped[s], child_codes_pool)
+            starts_block = r % RUNS_PER_BLOCK < RUNS_PER_PAIR
+            ends_kernel = r >= RUNS - RUNS_PER_PAIR
+            pair_sum = total if starts_block else first_child
+            if not last_run:
+                nc.vector.tensor_tensor(out=pair_sum, in0=first_child, in1=second_child, op=ADD)
+            if not starts_block and not ends_kernel:
+                for j in range(TWO):
+                    cols = slice(j * BLOCK_COLUMNS, (j + 1) * BLOCK_COLUMNS)
+                    nc.gpsimd.tensor_tensor(out=total[:, cols], in0=total[:, cols], in1=pair_sum[:, cols], op=ADD)
+            if ends_kernel:
+                for j in range(TWO):
+                    cols = slice(j * BLOCK_COLUMNS, (j + 1) * BLOCK_COLUMNS)
+                    terms = [total[:, cols], (second_child if last_run else first_child)[:, cols]]
+                    pending.append((TWO * half + j, terms))
 
-        for hb in range(H_BLOCKS):
-            store_block(
-                BLOCKS - 1, hb, [sums[BLOCKS - 1], products[STEPS - 3], products[STEPS - 1]], finish=hb == H_BLOCKS - 1
-            )
+        for hb, terms in pending:
+            store_block(BLOCKS - 1, hb, terms, split=hb >= TWO)

@@ -26,7 +26,8 @@ HALVES = WORDS // P
 H_BLOCK = PAIR * P
 H_BLOCKS = HIDDEN // H_BLOCK
 W_BOUNDS = (0, H_BLOCK, 2 * H_BLOCK, HIDDEN)
-PSUM_BANKS = 8
+CELL_BANKS = 4
+OTHER_BANKS = 4
 TWO = 2
 RUNS_PER_PAIR = H_BLOCKS // TWO
 RUNS_PER_BLOCK = CHILDREN // TWO * RUNS_PER_PAIR
@@ -58,7 +59,8 @@ def tile_childsumtreelstmcell_pa_t_kernel(tc, x, child_h, child_c, Wf, bWf, Uf, 
         prod_pool = ctx.enter_context(tc.tile_pool(name="prod", bufs=3))
         sum_pool = ctx.enter_context(tc.tile_pool(name="sums", bufs=BLOCKS))
         out_pool = ctx.enter_context(tc.tile_pool(name="out_rows", bufs=3))
-        banks_pool = ctx.enter_context(tc.psum_pool(name="banks", bufs=PSUM_BANKS))
+        banks_pool = ctx.enter_context(tc.psum_pool(name="banks", bufs=OTHER_BANKS))
+        cells_pool = ctx.enter_context(tc.psum_pool(name="cells", bufs=CELL_BANKS))
         ctx.enter_context(tc.manual_schedule())
 
         def load_weight_part(w, name, part):
@@ -162,7 +164,7 @@ def tile_childsumtreelstmcell_pa_t_kernel(tc, x, child_h, child_c, Wf, bWf, Uf, 
 
         def transpose_cells(rows, j):
             words = rows[:].bitcast(F32)
-            cells = banks_pool.tile([P, NODE_BLOCK], F32, name="cells", tag="bank")
+            cells = cells_pool.tile([P, NODE_BLOCK], F32, name="cells", tag="cells")
             for t in range(TILES):
                 first = (TWO * t + j) * P
                 nc.tensor.transpose(cells[:, t * P : (t + 1) * P], words[:, first : first + P], ident[:])

@@ -321,9 +321,9 @@ def tile_childsumtreelstmcell_pa_t_kernel(tc, x, child_h, child_c, Wf, bWf, Uf, 
             if r % RUNS_PER_BLOCK == X_RUN and b + 1 < BLOCKS:
                 grouped["node"] = regroup_rows(transpose_rows(x_rows[b + 1]))
 
-            if b > 0 and r % RUNS_PER_BLOCK < RUNS_PER_PAIR:
-                for hb in (TWO * half, TWO * half + 1):
-                    store_block(b - 1, hb, [sums[b - 1][:, sum_columns(hb)]])
+            out_hb = r % RUNS_PER_BLOCK - RUNS_PER_PAIR
+            if b > 0 and 0 <= out_hb < H_BLOCKS:
+                store_block(b - 1, out_hb, [sums[b - 1][:, sum_columns(out_hb)]])
 
             if r == 0:
                 for hb in range(TWO, H_BLOCKS):

@@ -348,13 +348,12 @@ def tile_childsumtreelstmcell_pa_t_kernel(tc, x, child_h, child_c, Wf, bWf, Uf, 
                     children[s] = quantise_rows(grouped[s], child_codes_pool)
             starts_block = r % RUNS_PER_BLOCK < RUNS_PER_PAIR
             ends_kernel = r >= RUNS - RUNS_PER_PAIR
-            pair_sum = total if starts_block else first_child
-            if not last_run:
-                nc.vector.tensor_tensor(out=pair_sum, in0=first_child, in1=second_child, op=ADD)
-            if not starts_block and not ends_kernel:
-                for j in range(TWO):
-                    cols = slice(j * BLOCK_COLUMNS, (j + 1) * BLOCK_COLUMNS)
-                    nc.gpsimd.tensor_tensor(out=total[:, cols], in0=total[:, cols], in1=pair_sum[:, cols], op=ADD)
+            if starts_block:
+                nc.gpsimd.tensor_tensor(out=total, in0=first_child, in1=second_child, op=ADD)
+            elif not last_run:
+                nc.vector.tensor_tensor(out=first_child, in0=first_child, in1=second_child, op=ADD)
+                if not ends_kernel:
+                    nc.gpsimd.tensor_tensor(out=total, in0=total, in1=first_child, op=ADD)
             if ends_kernel:
                 for j in range(TWO):
                     cols = slice(j * BLOCK_COLUMNS, (j + 1) * BLOCK_COLUMNS)

@@ -51,6 +51,7 @@ def tile_childsumtreelstmcell_pa_t_kernel(tc, x, child_h, child_c, Wf, bWf, Uf, 
         wstage = ctx.enter_context(tc.tile_pool(name="wstage", bufs=4))
         x_rows_pool = ctx.enter_context(tc.tile_pool(name="x_rows", bufs=BLOCKS))
         h_rows_pool = ctx.enter_context(tc.tile_pool(name="h_rows", bufs=4))
+        ordered_pool = ctx.enter_context(tc.tile_pool(name="ordered", bufs=2))
         c_rows_pool = ctx.enter_context(tc.tile_pool(name="c_rows", bufs=8))
         grouped_pool = ctx.enter_context(tc.tile_pool(name="grouped", bufs=3))
         child_codes_pool = ctx.enter_context(tc.tile_pool(name="child_codes", bufs=5))
@@ -114,7 +115,7 @@ def tile_childsumtreelstmcell_pa_t_kernel(tc, x, child_h, child_c, Wf, bWf, Uf, 
                 rows.append(cells)
             return rows
 
-        def transpose_rows(rows):
+        def transpose_rows(rows, ordered=False):
             words = rows[:].bitcast(F32)
             banks = []
             for half in range(TILES // 2):
@@ -122,9 +123,21 @@ def tile_childsumtreelstmcell_pa_t_kernel(tc, x, child_h, child_c, Wf, bWf, Uf, 
                 for a in range(2):
                     for u in range(HALVES):
                         first = (2 * half + a) * WORDS
-                        nc.tensor.transpose(bank[:, a, u, :], words[:, first + u : first + WORDS : HALVES], ident[:])
+                        if ordered:
+                            taken = slice(first + u * P, first + (u + 1) * P)
+                        else:
+                            taken = slice(first + u, first + WORDS, HALVES)
+                        nc.tensor.transpose(bank[:, a, u, :], words[:, taken], ident[:])
                 banks.append(bank)
             return banks
+
+        def order_words(rows):
+            ordered = ordered_pool.tile([P, TILES * FEATURES], BF16, name="ordered")
+            nc.scalar.copy(
+                out=ordered[:].bitcast(F32).rearrange("p (t u w) -> p t u w", t=TILES, u=HALVES),
+                in_=rows[:].bitcast(F32).rearrange("p (t w u) -> p t u w", t=TILES, u=HALVES),
+            )
+            return ordered
 
         def regroup_rows(banks):
             grouped = grouped_pool.tile([P, NODE_BLOCK * PACK], BF16, align_bytes=64)
@@ -239,6 +252,7 @@ def tile_childsumtreelstmcell_pa_t_kernel(tc, x, child_h, child_c, Wf, bWf, Uf, 
         h_rows[2] = load_child(2)
         c_rows[1] = load_cells(1)
         h_rows[3] = load_child(3)
+        h_rows[4] = load_child(4)
         c_rows[2] = load_cells(2)
         x_rows[1] = load_x(1)
 
@@ -273,17 +287,17 @@ def tile_childsumtreelstmcell_pa_t_kernel(tc, x, child_h, child_c, Wf, bWf, Uf, 
         quantise_weight_block(grouped_u, u_codes, u_scales, 1)
         quantise_weight_block(grouped_w, w_codes, w_scales, 1)
         sums = {}
+        ordered_rows = {}
         pending = []
 
         for r in range(RUNS):
             pair, half = divmod(r, RUNS_PER_PAIR)
             b = r // RUNS_PER_BLOCK
             units = [(j, i) for j in range(TWO) for i in range(TWO)]
-            prepare = r + 3
-            also = 2 if r == 0 else None
+            prepare = [2, 3] if r == 0 else [r + 3]
             last_run = r == RUNS - 1
-            if r + 4 < STEPS:
-                h_rows[r + 4] = load_child(r + 4)
+            if r + 5 < STEPS:
+                h_rows[r + 5] = load_child(r + 5)
             if r + 3 < RUNS:
                 c_rows[r + 3] = load_cells(r + 3)
 
@@ -315,9 +329,12 @@ def tile_childsumtreelstmcell_pa_t_kernel(tc, x, child_h, child_c, Wf, bWf, Uf, 
                         )
                     gates[(j, i)] = gate
 
-            for s in (also, prepare):
-                if s is not None and s < STEPS:
-                    grouped[s] = regroup_rows(transpose_rows(h_rows[s]))
+            if r > 0 and r + 4 < STEPS:
+                ordered_rows[r + 4] = order_words(h_rows[r + 4])
+            for s in prepare:
+                if s < STEPS:
+                    in_order = s in ordered_rows
+                    grouped[s] = regroup_rows(transpose_rows(ordered_rows[s] if in_order else h_rows[s], in_order))
             if r % RUNS_PER_BLOCK == X_RUN and b + 1 < BLOCKS:
                 grouped["node"] = regroup_rows(transpose_rows(x_rows[b + 1]))
 
@@ -343,7 +360,7 @@ def tile_childsumtreelstmcell_pa_t_kernel(tc, x, child_h, child_c, Wf, bWf, Uf, 
                     nc.gpsimd.tensor_tensor(out=total[:, cols], in0=total[:, cols], in1=first_child[:, cols], op=ADD)
             if "node" in grouped:
                 nodes[b + 1] = quantise_rows(grouped["node"], node_codes_pool)
-            for s in (also, prepare):
+            for s in prepare:
                 if s in grouped:
                     children[s] = quantise_rows(grouped[s], child_codes_pool)
             starts_block = r % RUNS_PER_BLOCK < RUNS_PER_PAIR

@@ -35,6 +35,12 @@ RUNS = BLOCKS * RUNS_PER_BLOCK
 STEPS = BLOCKS * CHILDREN
 BLOCK_COLUMNS = PAIR * NODE_BLOCK
 RUN_COLUMNS = TWO * BLOCK_COLUMNS
+RUN_ORDER = (
+    [(0, pair, half) for half in range(TWO) for pair in range(TWO)]
+    + [(0, pair, half) for pair in range(TWO, CHILDREN // TWO) for half in range(TWO)]
+    + [(b, pair, half) for b in range(1, BLOCKS) for pair in range(CHILDREN // TWO) for half in range(TWO)]
+)
+STORE_RUN = 3
 X_RUN = 3
 
 
@@ -52,14 +58,14 @@ def tile_childsumtreelstmcell_pa_t_kernel(tc, x, child_h, child_c, Wf, bWf, Uf, 
         x_rows_pool = ctx.enter_context(tc.tile_pool(name="x_rows", bufs=BLOCKS))
         h_rows_pool = ctx.enter_context(tc.tile_pool(name="h_rows", bufs=4))
         ordered_pool = ctx.enter_context(tc.tile_pool(name="ordered", bufs=2))
-        c_rows_pool = ctx.enter_context(tc.tile_pool(name="c_rows", bufs=8))
+        c_rows_pool = ctx.enter_context(tc.tile_pool(name="c_rows", bufs=6))
         grouped_pool = ctx.enter_context(tc.tile_pool(name="grouped", bufs=3))
-        child_codes_pool = ctx.enter_context(tc.tile_pool(name="child_codes", bufs=5))
+        child_codes_pool = ctx.enter_context(tc.tile_pool(name="child_codes", bufs=6))
         node_codes_pool = ctx.enter_context(tc.tile_pool(name="node_codes", bufs=BLOCKS))
         gate_pool = ctx.enter_context(tc.tile_pool(name="gate", bufs=6))
         prod_pool = ctx.enter_context(tc.tile_pool(name="prod", bufs=3))
         sum_pool = ctx.enter_context(tc.tile_pool(name="sums", bufs=BLOCKS))
-        out_pool = ctx.enter_context(tc.tile_pool(name="out_rows", bufs=3))
+        half_pool = ctx.enter_context(tc.tile_pool(name="half_rows", bufs=6))
         banks_pool = ctx.enter_context(tc.psum_pool(name="banks", bufs=OTHER_BANKS))
         cells_pool = ctx.enter_context(tc.psum_pool(name="cells", bufs=CELL_BANKS))
         ctx.enter_context(tc.manual_schedule())
@@ -67,7 +73,7 @@ def tile_childsumtreelstmcell_pa_t_kernel(tc, x, child_h, child_c, Wf, bWf, Uf, 
         def load_weight_part(w, name, part):
             cols = slice(W_BOUNDS[part], W_BOUNDS[part + 1])
             last = part == len(W_BOUNDS) - 2
-            pool, tag = (prod_pool, "products") if last else (weights, "raw_%s%d" % (name, part))
+            pool, tag = (c_rows_pool, "c_rows") if last else (weights, "raw_%s%d" % (name, part))
             raw = pool.tile([P, PACK * (cols.stop - cols.start)], BF16, name="raw", tag=tag)
             nc.sync.dma_start(
                 out=raw[:].rearrange("q (j c) -> q j c", j=PACK),
@@ -79,12 +85,11 @@ def tile_childsumtreelstmcell_pa_t_kernel(tc, x, child_h, child_c, Wf, bWf, Uf, 
             part = min(hb, len(W_BOUNDS) - 2)
             first = H_BLOCK * hb - W_BOUNDS[part]
             grouped_w = wstage.tile([P, H_BLOCK * PACK], BF16, align_bytes=64)
-            nc.vector.tensor_copy(
-                out=grouped_w[:].rearrange("q (e m j) -> q e m j", e=PAIR, j=PACK),
-                in_=raw_parts[part][:].rearrange("q (j c) -> q j c", j=PACK)[:, :, first : first + H_BLOCK].rearrange(
-                    "q j (m e) -> q e m j", e=PAIR
-                ),
+            grouped_view = grouped_w[:].rearrange("q (e m j) -> q e m j", e=PAIR, j=PACK)
+            raw_view = raw_parts[part][:].rearrange("q (j c) -> q j c", j=PACK)[:, :, first : first + H_BLOCK].rearrange(
+                "q j (m e) -> q e m j", e=PAIR
             )
+            nc.vector.tensor_copy(out=grouped_view, in_=raw_view)
             return grouped_w
 
         def quantise_weight_block(grouped_w, codes, scales, hb):
@@ -103,11 +108,10 @@ def tile_childsumtreelstmcell_pa_t_kernel(tc, x, child_h, child_c, Wf, bWf, Uf, 
             return rows
 
         def load_cells(r):
-            pair, half = divmod(r, RUNS_PER_PAIR)
+            b, pair, half = RUN_ORDER[r]
             rows = []
-            for s in (TWO * pair, TWO * pair + 1):
-                b, k = divmod(s, CHILDREN)
-                cells = c_rows_pool.tile([P, TILES * TWO * H_BLOCK], BF16, name="c_rows")
+            for k in (TWO * pair, TWO * pair + 1):
+                cells = c_rows_pool.tile([P, TILES * TWO * H_BLOCK], BF16, name="c_rows", tag="c_rows")
                 nc.sync.dma_start(
                     out=cells[:].rearrange("p (t h) -> p t h", t=TILES),
                     in_=c_view[b, :, :, k, TWO * H_BLOCK * half : TWO * H_BLOCK * (half + 1)],
@@ -191,35 +195,31 @@ def tile_childsumtreelstmcell_pa_t_kernel(tc, x, child_h, child_c, Wf, bWf, Uf, 
                 op=MULT,
             )
 
-        def store_block(b, hb, terms, split=False):
-            rows = out_pool.tile([P, TILES * H_BLOCK], F32, name="out_rows")
-            rows_view = rows[:].rearrange("p (h a w e) -> p h a w e", h=2, a=2, e=PAIR)
-            out_rows = rows[:].rearrange("p (t h) -> p t h", t=TILES)
-            out_cols = slice(H_BLOCK * hb, H_BLOCK * (hb + 1))
-            for half in range(TILES // 2):
-                bank = banks_pool.tile([P, 2, PAIR, P], F32, name="bank", tag="bank")
-                for a in range(2):
-                    for e in range(PAIR):
-                        first = e * NODE_BLOCK + (2 * half + a) * P
-                        for i, term in enumerate(terms):
-                            nc.tensor.matmul(
-                                bank[:, a, e, :],
-                                lhsT=term[:, first : first + P],
-                                rhs=ident[:],
-                                start=i == 0,
-                                stop=i == len(terms) - 1,
-                                is_transpose=True,
-                            )
-                bank_view = bank[:].rearrange("p a e w -> p a w e")
-                if split and half == 1:
-                    nc.vector.tensor_copy(out=rows_view[:, half], in_=bank_view)
-                else:
-                    nc.scalar.copy(out=rows_view[:, half], in_=bank_view)
-                if split:
-                    two = slice(2 * half, 2 * half + 2)
-                    nc.sync.dma_start(out=out_view[b, :, two, out_cols], in_=out_rows[:, two, :])
-            if not split:
-                nc.sync.dma_start(out=out_view[b, :, :, out_cols], in_=out_rows)
+        def store_half(b, hb, half, terms, engine="scalar"):
+            rows = half_pool.tile([P, TILES // 2 * H_BLOCK], F32, name="half_rows")
+            bank = banks_pool.tile([P, 2, PAIR, P], F32, name="bank", tag="bank")
+            for a in range(2):
+                for e in range(PAIR):
+                    first = e * NODE_BLOCK + (2 * half + a) * P
+                    for i, term in enumerate(terms):
+                        nc.tensor.matmul(
+                            bank[:, a, e, :],
+                            lhsT=term[:, first : first + P],
+                            rhs=ident[:],
+                            start=i == 0,
+                            stop=i == len(terms) - 1,
+                            is_transpose=True,
+                        )
+            rows_view = rows[:].rearrange("p (a w e) -> p a w e", a=2, e=PAIR)
+            bank_view = bank[:].rearrange("p a e w -> p a w e")
+            if engine == "scalar":
+                nc.scalar.copy(out=rows_view, in_=bank_view)
+            else:
+                nc.vector.tensor_copy(out=rows_view, in_=bank_view)
+            nc.sync.dma_start(
+                out=out_view[b, :, 2 * half : 2 * half + 2, H_BLOCK * hb : H_BLOCK * (hb + 1)],
+                in_=rows[:].rearrange("p (t h) -> p t h", t=TILES // 2),
+            )
 
         def sum_columns(hb):
             return slice(hb * BLOCK_COLUMNS, (hb + 1) * BLOCK_COLUMNS)
@@ -230,8 +230,10 @@ def tile_childsumtreelstmcell_pa_t_kernel(tc, x, child_h, child_c, Wf, bWf, Uf, 
         bias_rows = const.tile([P, P], F32)
         nc.vector.memset(bias_rows[:], 0.0)
         bias_rows_bf = bias_rows[:].bitcast(BF16)
-        nc.sync.dma_start(out=bias_rows_bf[0:H_BLOCKS, :], in_=bWf.rearrange("(r c) -> r c", c=H_BLOCK))
-        nc.sync.dma_start(out=bias_rows_bf[H_BLOCKS : 2 * H_BLOCKS, :], in_=bUf.rearrange("(r c) -> r c", c=H_BLOCK))
+
+        def load_biases():
+            nc.sync.dma_start(out=bias_rows_bf[0:H_BLOCKS, :], in_=bWf.rearrange("(r c) -> r c", c=H_BLOCK))
+            nc.sync.dma_start(out=bias_rows_bf[H_BLOCKS : 2 * H_BLOCKS, :], in_=bUf.rearrange("(r c) -> r c", c=H_BLOCK))
 
         first_sigmoid = const.tile([P, 1], F32)
         nc.vector.memset(first_sigmoid[:], 0.0)
@@ -239,19 +241,23 @@ def tile_childsumtreelstmcell_pa_t_kernel(tc, x, child_h, child_c, Wf, bWf, Uf, 
 
         u_raw = {}
         w_raw = {}
-        h_rows = {0: load_child(0)}
+        h_rows = {}
+        x_rows = {}
+        c_rows = {}
+        h_rows[0] = load_child(0)
+        x_rows[0] = load_x(0)
         u_raw[0] = load_weight_part(Uf, "u", 0)
-        x_rows = {0: load_x(0)}
         w_raw[0] = load_weight_part(Wf, "w", 0)
+        load_biases()
         h_rows[1] = load_child(1)
         u_raw[1] = load_weight_part(Uf, "u", 1)
         w_raw[1] = load_weight_part(Wf, "w", 1)
-        c_rows = {0: load_cells(0)}
+        c_rows[0] = load_cells(0)
+        h_rows[2] = load_child(2)
+        h_rows[3] = load_child(3)
+        c_rows[1] = load_cells(1)
         u_raw[2] = load_weight_part(Uf, "u", 2)
         w_raw[2] = load_weight_part(Wf, "w", 2)
-        h_rows[2] = load_child(2)
-        c_rows[1] = load_cells(1)
-        h_rows[3] = load_child(3)
         h_rows[4] = load_child(4)
         c_rows[2] = load_cells(2)
         x_rows[1] = load_x(1)
@@ -266,11 +272,11 @@ def tile_childsumtreelstmcell_pa_t_kernel(tc, x, child_h, child_c, Wf, bWf, Uf, 
         grouped_h0 = regroup_rows(banks_h0)
         grouped_x0 = regroup_rows(banks_x0)
         grouped_u = regroup_weight_block(u_raw, 0)
-        grouped_w = regroup_weight_block(w_raw, 0)
         children = {0: quantise_rows(grouped_h0, child_codes_pool)}
         quantise_weight_block(grouped_u, u_codes, u_scales, 0)
-        quantise_weight_block(grouped_w, w_codes, w_scales, 0)
+        grouped_w = regroup_weight_block(w_raw, 0)
         nodes = {0: quantise_rows(grouped_x0, node_codes_pool)}
+        quantise_weight_block(grouped_w, w_codes, w_scales, 0)
 
         bias_ps = banks_pool.tile([P, P], F32, name="bias_ps", tag="bank")
         nc.tensor.transpose(bias_ps[:], bias_rows[:], ident[:])
@@ -286,36 +292,40 @@ def tile_childsumtreelstmcell_pa_t_kernel(tc, x, child_h, child_c, Wf, bWf, Uf, 
         grouped_w = regroup_weight_block(w_raw, 1)
         quantise_weight_block(grouped_u, u_codes, u_scales, 1)
         quantise_weight_block(grouped_w, w_codes, w_scales, 1)
+        def prepare_weight_block(hb):
+            grouped_u = regroup_weight_block(u_raw, hb)
+            grouped_w = regroup_weight_block(w_raw, hb)
+            quantise_weight_block(grouped_u, u_codes, u_scales, hb)
+            quantise_weight_block(grouped_w, w_codes, w_scales, hb)
+
         sums = {}
         ordered_rows = {}
         pending = []
 
         for r in range(RUNS):
-            pair, half = divmod(r, RUNS_PER_PAIR)
-            b = r // RUNS_PER_BLOCK
+            b, pair, half = RUN_ORDER[r]
+            first_step = b * CHILDREN + TWO * pair
             units = [(j, i) for j in range(TWO) for i in range(TWO)]
+            if r == 1:
+                units = [(j, i) for i in range(TWO) for j in range(TWO)]
             prepare = [2, 3] if r == 0 else [r + 3]
             last_run = r == RUNS - 1
             if r + 5 < STEPS:
                 h_rows[r + 5] = load_child(r + 5)
-            if r + 3 < RUNS:
-                c_rows[r + 3] = load_cells(r + 3)
+            if r + 2 < RUNS and r + 2 not in c_rows:
+                c_rows[r + 2] = load_cells(r + 2)
 
             z = {}
             cells = {}
             gates = {}
             grouped = {}
-            groups = [units[:2], units[2:]] if last_run else [units]
+            groups = [units[:2], units[2:]] if last_run or r == 0 else [units]
             for g, group in enumerate(groups):
-                if last_run:
-                    for j, i in group:
-                        cells[(j, i)] = transpose_cells(c_rows[r][i], j)
                 for j, i in group:
                     for e in range(PAIR):
-                        z[(j, i, e)] = gate_sums(TWO * half + j, e, children[TWO * pair + i], nodes[b])
-                if not last_run:
-                    for j, i in group:
-                        cells[(j, i)] = transpose_cells(c_rows[r][i], j)
+                        z[(j, i, e)] = gate_sums(TWO * half + j, e, children[first_step + i], nodes[b])
+                for j, i in group:
+                    cells[(j, i)] = transpose_cells(c_rows[r][i], j)
                 for j, i in group:
                     gate = gate_pool.tile([P, BLOCK_COLUMNS], F32)
                     for e in range(PAIR):
@@ -329,7 +339,7 @@ def tile_childsumtreelstmcell_pa_t_kernel(tc, x, child_h, child_c, Wf, bWf, Uf, 
                         )
                     gates[(j, i)] = gate
 
-            if r > 0 and r + 4 < STEPS:
+            if r >= 1 and r + 4 < STEPS:
                 ordered_rows[r + 4] = order_words(h_rows[r + 4])
             for s in prepare:
                 if s < STEPS:
@@ -338,34 +348,32 @@ def tile_childsumtreelstmcell_pa_t_kernel(tc, x, child_h, child_c, Wf, bWf, Uf, 
             if r % RUNS_PER_BLOCK == X_RUN and b + 1 < BLOCKS:
                 grouped["node"] = regroup_rows(transpose_rows(x_rows[b + 1]))
 
-            out_hb = r % RUNS_PER_BLOCK - RUNS_PER_PAIR
-            if b > 0 and 0 <= out_hb < H_BLOCKS:
-                store_block(b - 1, out_hb, [sums[b - 1][:, sum_columns(out_hb)]])
+            out_hb = r - RUNS_PER_BLOCK - STORE_RUN
+            if 0 <= out_hb < H_BLOCKS:
+                for n in range(TILES // 2):
+                    store_half(b - 1, out_hb, n, [sums[b - 1][:, sum_columns(out_hb)]])
 
-            if r == 0:
-                for hb in range(TWO, H_BLOCKS):
-                    grouped_u = regroup_weight_block(u_raw, hb)
-                    grouped_w = regroup_weight_block(w_raw, hb)
-                    quantise_weight_block(grouped_u, u_codes, u_scales, hb)
-                    quantise_weight_block(grouped_w, w_codes, w_scales, hb)
             if r % RUNS_PER_BLOCK == 0:
                 sums[b] = sum_pool.tile([P, H_BLOCKS * BLOCK_COLUMNS], F32, name="total")
             products = prod_pool.tile([P, TWO * RUN_COLUMNS], F32, name="products", tag="products")
             first_child, second_child = products[:, 0:RUN_COLUMNS], products[:, RUN_COLUMNS : 2 * RUN_COLUMNS]
             total = sums[b][:, half * RUN_COLUMNS : (half + 1) * RUN_COLUMNS]
-            for j, i in units:
+            for n, (j, i) in enumerate(units):
+                if r == 0 and n == len(units) - 1:
+                    children[2] = quantise_rows(grouped.pop(2), child_codes_pool)
                 multiply(products, TWO * i + j, gates[(j, i)], cells[(j, i)])
-                if last_run and i == 0:
-                    cols = slice(j * BLOCK_COLUMNS, (j + 1) * BLOCK_COLUMNS)
-                    nc.gpsimd.tensor_tensor(out=total[:, cols], in0=total[:, cols], in1=first_child[:, cols], op=ADD)
             if "node" in grouped:
                 nodes[b + 1] = quantise_rows(grouped["node"], node_codes_pool)
             for s in prepare:
                 if s in grouped:
                     children[s] = quantise_rows(grouped[s], child_codes_pool)
-            starts_block = r % RUNS_PER_BLOCK < RUNS_PER_PAIR
+            if r == 0:
+                for hb in range(TWO, H_BLOCKS):
+                    prepare_weight_block(hb)
             ends_kernel = r >= RUNS - RUNS_PER_PAIR
-            if starts_block:
+            if pair == 0:
+                if b == 0:
+                    nc.vector.memset(total[:, 0:1], 0.0)
                 nc.gpsimd.tensor_tensor(out=total, in0=first_child, in1=second_child, op=ADD)
             elif not last_run:
                 nc.vector.tensor_tensor(out=first_child, in0=first_child, in1=second_child, op=ADD)
@@ -374,8 +382,11 @@ def tile_childsumtreelstmcell_pa_t_kernel(tc, x, child_h, child_c, Wf, bWf, Uf, 
             if ends_kernel:
                 for j in range(TWO):
                     cols = slice(j * BLOCK_COLUMNS, (j + 1) * BLOCK_COLUMNS)
-                    terms = [total[:, cols], (second_child if last_run else first_child)[:, cols]]
+                    terms = [total[:, cols], first_child[:, cols]]
+                    if last_run:
+                        terms.append(second_child[:, cols])
                     pending.append((TWO * half + j, terms))
 
         for hb, terms in pending:
-            store_block(BLOCKS - 1, hb, terms, split=hb >= TWO)
+            for half in range(TILES // 2):
+                store_half(BLOCKS - 1, hb, half, terms, "scalar" if hb < TWO or half == 0 else "vector")

@@ -197,6 +197,8 @@ def tile_childsumtreelstmcell_pa_t_kernel(tc, x, child_h, child_c, Wf, bWf, Uf, 
 
         def store_half(b, hb, half, terms, engine="scalar"):
             rows = half_pool.tile([P, TILES // 2 * H_BLOCK], F32, name="half_rows")
+            if b == BLOCKS - 1:
+                keep_clock_up(1)
             bank = banks_pool.tile([P, 2, PAIR, P], F32, name="bank", tag="bank")
             for a in range(2):
                 for e in range(PAIR):
@@ -235,6 +237,14 @@ def tile_childsumtreelstmcell_pa_t_kernel(tc, x, child_h, child_c, Wf, bWf, Uf, 
             nc.sync.dma_start(out=bias_rows_bf[0:H_BLOCKS, :], in_=bWf.rearrange("(r c) -> r c", c=H_BLOCK))
             nc.sync.dma_start(out=bias_rows_bf[H_BLOCKS : 2 * H_BLOCKS, :], in_=bUf.rearrange("(r c) -> r c", c=H_BLOCK))
 
+        zeros = const.tile([P, NODE_BLOCK], BF16)
+        nc.vector.memset(zeros[:], 0.0)
+
+        def keep_clock_up(count):
+            unused = banks_pool.tile([P, NODE_BLOCK], F32, name="unused", tag="bank")
+            for n in range(count):
+                nc.tensor.matmul(unused[:], lhsT=zeros[:, 0:P], rhs=zeros[:], start=True, stop=True)
+
         first_sigmoid = const.tile([P, 1], F32)
         nc.vector.memset(first_sigmoid[:], 0.0)
         nc.scalar.activation(out=first_sigmoid[:], in_=first_sigmoid[:], func=SIGMOID)
@@ -267,8 +277,11 @@ def tile_childsumtreelstmcell_pa_t_kernel(tc, x, child_h, child_c, Wf, bWf, Uf, 
         w_codes = weights.tile([P, HIDDEN], U32, align_bytes=64)
         w_scales = weights.tile([P, HIDDEN], U8, align_bytes=64)
 
+        keep_clock_up(7)
         banks_h0 = transpose_rows(h_rows[0])
+        keep_clock_up(2)
         banks_x0 = transpose_rows(x_rows[0])
+        keep_clock_up(4)
         grouped_h0 = regroup_rows(banks_h0)
         grouped_x0 = regroup_rows(banks_x0)
         grouped_u = regroup_weight_block(u_raw, 0)
@@ -281,6 +294,7 @@ def tile_childsumtreelstmcell_pa_t_kernel(tc, x, child_h, child_c, Wf, bWf, Uf, 
         bias_ps = banks_pool.tile([P, P], F32, name="bias_ps", tag="bank")
         nc.tensor.transpose(bias_ps[:], bias_rows[:], ident[:])
         grouped_h1 = regroup_rows(transpose_rows(h_rows[1]))
+        keep_clock_up(1)
         both = const.tile([P, 2 * PAIR * H_BLOCKS], F32)
         nc.vector.tensor_copy(out=both[:], in_=bias_ps[:, 0 : 2 * H_BLOCKS].bitcast(BF16))
         bias = const.tile([P, PAIR * H_BLOCKS], F32)
@@ -321,6 +335,8 @@ def tile_childsumtreelstmcell_pa_t_kernel(tc, x, child_h, child_c, Wf, bWf, Uf, 
             grouped = {}
             groups = [units[:2], units[2:]] if last_run or r == 0 else [units]
             for g, group in enumerate(groups):
+                if last_run:
+                    keep_clock_up(2)
                 for j, i in group:
                     for e in range(PAIR):
                         z[(j, i, e)] = gate_sums(TWO * half + j, e, children[first_step + i], nodes[b])
@@ -342,6 +358,8 @@ def tile_childsumtreelstmcell_pa_t_kernel(tc, x, child_h, child_c, Wf, bWf, Uf, 
             if r >= 1 and r + 4 < STEPS:
                 ordered_rows[r + 4] = order_words(h_rows[r + 4])
             for s in prepare:
+                if r == 0:
+                    keep_clock_up(s - 1)
                 if s < STEPS:
                     in_order = s in ordered_rows
                     grouped[s] = regroup_rows(transpose_rows(ordered_rows[s] if in_order else h_rows[s], in_order))

@@ -197,8 +197,6 @@ def tile_childsumtreelstmcell_pa_t_kernel(tc, x, child_h, child_c, Wf, bWf, Uf, 
 
         def store_half(b, hb, half, terms, engine="scalar"):
             rows = half_pool.tile([P, TILES // 2 * H_BLOCK], F32, name="half_rows")
-            if b == BLOCKS - 1:
-                keep_clock_up(1)
             bank = banks_pool.tile([P, 2, PAIR, P], F32, name="bank", tag="bank")
             for a in range(2):
                 for e in range(PAIR):
@@ -335,8 +333,6 @@ def tile_childsumtreelstmcell_pa_t_kernel(tc, x, child_h, child_c, Wf, bWf, Uf, 
             grouped = {}
             groups = [units[:2], units[2:]] if last_run or r == 0 else [units]
             for g, group in enumerate(groups):
-                if last_run:
-                    keep_clock_up(2)
                 for j, i in group:
                     for e in range(PAIR):
                         z[(j, i, e)] = gate_sums(TWO * half + j, e, children[first_step + i], nodes[b])
@@ -355,12 +351,13 @@ def tile_childsumtreelstmcell_pa_t_kernel(tc, x, child_h, child_c, Wf, bWf, Uf, 
                         )
                     gates[(j, i)] = gate
 
+                if r == 0 and g == 0:
+                    grouped[2] = regroup_rows(transpose_rows(h_rows[2]))
+
             if r >= 1 and r + 4 < STEPS:
                 ordered_rows[r + 4] = order_words(h_rows[r + 4])
             for s in prepare:
-                if r == 0:
-                    keep_clock_up(s - 1)
-                if s < STEPS:
+                if s < STEPS and s not in grouped:
                     in_order = s in ordered_rows
                     grouped[s] = regroup_rows(transpose_rows(ordered_rows[s] if in_order else h_rows[s], in_order))
             if r % RUNS_PER_BLOCK == X_RUN and b + 1 < BLOCKS:
@@ -377,7 +374,7 @@ def tile_childsumtreelstmcell_pa_t_kernel(tc, x, child_h, child_c, Wf, bWf, Uf, 
             first_child, second_child = products[:, 0:RUN_COLUMNS], products[:, RUN_COLUMNS : 2 * RUN_COLUMNS]
             total = sums[b][:, half * RUN_COLUMNS : (half + 1) * RUN_COLUMNS]
             for n, (j, i) in enumerate(units):
-                if r == 0 and n == len(units) - 1:
+                if r == 0 and n == 2:
                     children[2] = quantise_rows(grouped.pop(2), child_codes_pool)
                 multiply(products, TWO * i + j, gates[(j, i)], cells[(j, i)])
             if "node" in grouped:
@@ -394,7 +391,10 @@ def tile_childsumtreelstmcell_pa_t_kernel(tc, x, child_h, child_c, Wf, bWf, Uf, 
                     nc.vector.memset(total[:, 0:1], 0.0)
                 nc.gpsimd.tensor_tensor(out=total, in0=first_child, in1=second_child, op=ADD)
             elif not last_run:
-                nc.vector.tensor_tensor(out=first_child, in0=first_child, in1=second_child, op=ADD)
+                parts = 1 if prepare[0] < STEPS else TWO
+                for j in range(parts):
+                    cols = slice(j * RUN_COLUMNS // parts, (j + 1) * RUN_COLUMNS // parts)
+                    nc.vector.tensor_tensor(out=first_child[:, cols], in0=first_child[:, cols], in1=second_child[:, cols], op=ADD)
                 if not ends_kernel:
                     nc.gpsimd.tensor_tensor(out=total, in0=total, in1=first_child, op=ADD)
             if ends_kernel:
@@ -405,6 +405,7 @@ def tile_childsumtreelstmcell_pa_t_kernel(tc, x, child_h, child_c, Wf, bWf, Uf, 
                         terms.append(second_child[:, cols])
                     pending.append((TWO * half + j, terms))
 
+        keep_clock_up(3)
         for hb, terms in pending:
             for half in range(TILES // 2):
                 store_half(BLOCKS - 1, hb, half, terms, "scalar" if hb < TWO or half == 0 else "vector")

@@ -275,7 +275,7 @@ def tile_childsumtreelstmcell_pa_t_kernel(tc, x, child_h, child_c, Wf, bWf, Uf, 
         w_codes = weights.tile([P, HIDDEN], U32, align_bytes=64)
         w_scales = weights.tile([P, HIDDEN], U8, align_bytes=64)
 
-        keep_clock_up(7)
+        keep_clock_up(12)
         banks_h0 = transpose_rows(h_rows[0])
         keep_clock_up(2)
         banks_x0 = transpose_rows(x_rows[0])
@@ -354,6 +354,8 @@ def tile_childsumtreelstmcell_pa_t_kernel(tc, x, child_h, child_c, Wf, bWf, Uf, 
                 if r == 0 and g == 0:
                     grouped[2] = regroup_rows(transpose_rows(h_rows[2]))
 
+            if abs(r - RUNS_PER_BLOCK) <= 1:
+                keep_clock_up(1)
             if r >= 1 and r + 4 < STEPS:
                 ordered_rows[r + 4] = order_words(h_rows[r + 4])
             for s in prepare:
@@ -405,7 +407,8 @@ def tile_childsumtreelstmcell_pa_t_kernel(tc, x, child_h, child_c, Wf, bWf, Uf, 
                         terms.append(second_child[:, cols])
                     pending.append((TWO * half + j, terms))
 
-        keep_clock_up(3)
+        keep_clock_up(2)
         for hb, terms in pending:
+            keep_clock_up(1)
             for half in range(TILES // 2):
                 store_half(BLOCKS - 1, hb, half, terms, "scalar" if hb < TWO or half == 0 else "vector")

@@ -25,7 +25,7 @@ WORDS = FEATURES // PAIR
 HALVES = WORDS // P
 H_BLOCK = PAIR * P
 H_BLOCKS = HIDDEN // H_BLOCK
-W_BOUNDS = (0, H_BLOCK, 2 * H_BLOCK, HIDDEN)
+W_BOUNDS = (0, 2 * H_BLOCK, HIDDEN)
 CELL_BANKS = 4
 OTHER_BANKS = 4
 TWO = 2
@@ -47,7 +47,7 @@ X_RUN = 3
 def tile_childsumtreelstmcell_pa_t_kernel(tc, x, child_h, child_c, Wf, bWf, Uf, bUf, out):
     nc = tc.nc
     x_view = x.rearrange("(b p t) d -> b p (t d)", b=BLOCKS, t=TILES)
-    h_view = child_h.rearrange("(b p t) k d -> b p t k d", b=BLOCKS, t=TILES)
+    h_view = child_h.rearrange("(b p t) (q i) d -> b p t q (i d)", b=BLOCKS, t=TILES, i=TWO)
     c_view = child_c.rearrange("(b p t) k h -> b p t k h", b=BLOCKS, t=TILES)
     out_view = out.rearrange("(b p t) h -> b p t h", b=BLOCKS, t=TILES)
 
@@ -55,8 +55,8 @@ def tile_childsumtreelstmcell_pa_t_kernel(tc, x, child_h, child_c, Wf, bWf, Uf, 
         const = ctx.enter_context(tc.tile_pool(name="const", bufs=1))
         weights = ctx.enter_context(tc.tile_pool(name="weights", bufs=1))
         wstage = ctx.enter_context(tc.tile_pool(name="wstage", bufs=4))
-        x_rows_pool = ctx.enter_context(tc.tile_pool(name="x_rows", bufs=BLOCKS))
-        h_rows_pool = ctx.enter_context(tc.tile_pool(name="h_rows", bufs=4))
+        x_rows_pool = ctx.enter_context(tc.tile_pool(name="x_rows", bufs=1))
+        h_rows_pool = ctx.enter_context(tc.tile_pool(name="h_rows", bufs=3))
         ordered_pool = ctx.enter_context(tc.tile_pool(name="ordered", bufs=2))
         c_rows_pool = ctx.enter_context(tc.tile_pool(name="c_rows", bufs=6))
         grouped_pool = ctx.enter_context(tc.tile_pool(name="grouped", bufs=3))
@@ -82,7 +82,7 @@ def tile_childsumtreelstmcell_pa_t_kernel(tc, x, child_h, child_c, Wf, bWf, Uf, 
             return raw
 
         def regroup_weight_block(raw_parts, hb):
-            part = min(hb, len(W_BOUNDS) - 2)
+            part = hb // TWO
             first = H_BLOCK * hb - W_BOUNDS[part]
             grouped_w = wstage.tile([P, H_BLOCK * PACK], BF16, align_bytes=64)
             grouped_view = grouped_w[:].rearrange("q (e m j) -> q e m j", e=PAIR, j=PACK)
@@ -99,13 +99,15 @@ def tile_childsumtreelstmcell_pa_t_kernel(tc, x, child_h, child_c, Wf, bWf, Uf, 
         def load_x(b):
             rows = x_rows_pool.tile([P, TILES * FEATURES], BF16, name="x_rows")
             nc.sync.dma_start(out=rows[:], in_=x_view[b])
-            return rows
+            return rows[:].bitcast(F32).rearrange("p (t w) -> p t w", t=TILES)
 
-        def load_child(s):
+        def load_child_pair(s):
             b, k = divmod(s, CHILDREN)
-            rows = h_rows_pool.tile([P, TILES * FEATURES], BF16, name="h_rows")
-            nc.sync.dma_start(out=rows[:].rearrange("p (t d) -> p t d", t=TILES), in_=h_view[b, :, :, k, :])
-            return rows
+            rows = h_rows_pool.tile([P, TILES * TWO * FEATURES], BF16, name="h_rows")
+            nc.sync.dma_start(out=rows[:].rearrange("p (t f) -> p t f", t=TILES), in_=h_view[b, :, :, k // TWO, :])
+            words = rows[:].bitcast(F32).rearrange("p (t i w) -> p t i w", t=TILES, i=TWO)
+            for i in range(TWO):
+                h_rows[s + i] = words[:, :, i, :]
 
         def load_cells(r):
             b, pair, half = RUN_ORDER[r]
@@ -119,29 +121,24 @@ def tile_childsumtreelstmcell_pa_t_kernel(tc, x, child_h, child_c, Wf, bWf, Uf, 
                 rows.append(cells)
             return rows
 
-        def transpose_rows(rows, ordered=False):
-            words = rows[:].bitcast(F32)
+        def transpose_rows(words, ordered=False):
             banks = []
             for half in range(TILES // 2):
                 bank = banks_pool.tile([P, 2, HALVES, P], F32, name="bank", tag="bank")
                 for a in range(2):
                     for u in range(HALVES):
-                        first = (2 * half + a) * WORDS
-                        if ordered:
-                            taken = slice(first + u * P, first + (u + 1) * P)
-                        else:
-                            taken = slice(first + u, first + WORDS, HALVES)
-                        nc.tensor.transpose(bank[:, a, u, :], words[:, taken], ident[:])
+                        taken = slice(u * P, (u + 1) * P) if ordered else slice(u, WORDS, HALVES)
+                        nc.tensor.transpose(bank[:, a, u, :], words[:, 2 * half + a, taken], ident[:])
                 banks.append(bank)
             return banks
 
-        def order_words(rows):
+        def order_words(words):
             ordered = ordered_pool.tile([P, TILES * FEATURES], BF16, name="ordered")
             nc.scalar.copy(
                 out=ordered[:].bitcast(F32).rearrange("p (t u w) -> p t u w", t=TILES, u=HALVES),
-                in_=rows[:].bitcast(F32).rearrange("p (t w u) -> p t u w", t=TILES, u=HALVES),
+                in_=words.rearrange("p t (w u) -> p t u w", u=HALVES),
             )
-            return ordered
+            return ordered[:].bitcast(F32).rearrange("p (t w) -> p t w", t=TILES)
 
         def regroup_rows(banks):
             grouped = grouped_pool.tile([P, NODE_BLOCK * PACK], BF16, align_bytes=64)
@@ -252,21 +249,17 @@ def tile_childsumtreelstmcell_pa_t_kernel(tc, x, child_h, child_c, Wf, bWf, Uf, 
         h_rows = {}
         x_rows = {}
         c_rows = {}
-        h_rows[0] = load_child(0)
+        load_child_pair(0)
         x_rows[0] = load_x(0)
         u_raw[0] = load_weight_part(Uf, "u", 0)
         w_raw[0] = load_weight_part(Wf, "w", 0)
         load_biases()
-        h_rows[1] = load_child(1)
+        c_rows[0] = load_cells(0)
+        load_child_pair(2)
+        c_rows[1] = load_cells(1)
         u_raw[1] = load_weight_part(Uf, "u", 1)
         w_raw[1] = load_weight_part(Wf, "w", 1)
-        c_rows[0] = load_cells(0)
-        h_rows[2] = load_child(2)
-        h_rows[3] = load_child(3)
-        c_rows[1] = load_cells(1)
-        u_raw[2] = load_weight_part(Uf, "u", 2)
-        w_raw[2] = load_weight_part(Wf, "w", 2)
-        h_rows[4] = load_child(4)
+        load_child_pair(4)
         c_rows[2] = load_cells(2)
         x_rows[1] = load_x(1)
 
@@ -279,7 +272,7 @@ def tile_childsumtreelstmcell_pa_t_kernel(tc, x, child_h, child_c, Wf, bWf, Uf, 
         banks_h0 = transpose_rows(h_rows[0])
         keep_clock_up(2)
         banks_x0 = transpose_rows(x_rows[0])
-        keep_clock_up(4)
+        keep_clock_up(2)
         grouped_h0 = regroup_rows(banks_h0)
         grouped_x0 = regroup_rows(banks_x0)
         grouped_u = regroup_weight_block(u_raw, 0)
@@ -322,8 +315,8 @@ def tile_childsumtreelstmcell_pa_t_kernel(tc, x, child_h, child_c, Wf, bWf, Uf, 
                 units = [(j, i) for i in range(TWO) for j in range(TWO)]
             prepare = [2, 3] if r == 0 else [r + 3]
             last_run = r == RUNS - 1
-            if r + 5 < STEPS:
-                h_rows[r + 5] = load_child(r + 5)
+            if r % TWO == 0 and r + 6 < STEPS:
+                load_child_pair(r + 6)
             if r + 2 < RUNS and r + 2 not in c_rows:
                 c_rows[r + 2] = load_cells(r + 2)
 
@@ -354,8 +347,6 @@ def tile_childsumtreelstmcell_pa_t_kernel(tc, x, child_h, child_c, Wf, bWf, Uf, 
                 if r == 0 and g == 0:
                     grouped[2] = regroup_rows(transpose_rows(h_rows[2]))
 
-            if abs(r - RUNS_PER_BLOCK) <= 1:
-                keep_clock_up(1)
             if r >= 1 and r + 4 < STEPS:
                 ordered_rows[r + 4] = order_words(h_rows[r + 4])
             for s in prepare:
@@ -379,6 +370,9 @@ def tile_childsumtreelstmcell_pa_t_kernel(tc, x, child_h, child_c, Wf, bWf, Uf, 
                 if r == 0 and n == 2:
                     children[2] = quantise_rows(grouped.pop(2), child_codes_pool)
                 multiply(products, TWO * i + j, gates[(j, i)], cells[(j, i)])
+                if last_run and i == 0:
+                    cols = slice(j * BLOCK_COLUMNS, (j + 1) * BLOCK_COLUMNS)
+                    nc.gpsimd.tensor_tensor(out=total[:, cols], in0=total[:, cols], in1=first_child[:, cols], op=ADD)
             if "node" in grouped:
                 nodes[b + 1] = quantise_rows(grouped["node"], node_codes_pool)
             for s in prepare:
@@ -402,13 +396,10 @@ def tile_childsumtreelstmcell_pa_t_kernel(tc, x, child_h, child_c, Wf, bWf, Uf, 
             if ends_kernel:
                 for j in range(TWO):
                     cols = slice(j * BLOCK_COLUMNS, (j + 1) * BLOCK_COLUMNS)
-                    terms = [total[:, cols], first_child[:, cols]]
-                    if last_run:
-                        terms.append(second_child[:, cols])
+                    terms = [total[:, cols], (second_child if last_run else first_child)[:, cols]]
                     pending.append((TWO * half + j, terms))
 
-        keep_clock_up(2)
         for hb, terms in pending:
-            keep_clock_up(1)
+            keep_clock_up(2)
             for half in range(TILES // 2):
                 store_half(BLOCKS - 1, hb, half, terms, "scalar" if hb < TWO or half == 0 else "vector")

@@ -250,10 +250,10 @@ def tile_childsumtreelstmcell_pa_t_kernel(tc, x, child_h, child_c, Wf, bWf, Uf, 
         x_rows = {}
         c_rows = {}
         load_child_pair(0)
+        load_biases()
         x_rows[0] = load_x(0)
         u_raw[0] = load_weight_part(Uf, "u", 0)
         w_raw[0] = load_weight_part(Wf, "w", 0)
-        load_biases()
         c_rows[0] = load_cells(0)
         load_child_pair(2)
         c_rows[1] = load_cells(1)
@@ -370,9 +370,6 @@ def tile_childsumtreelstmcell_pa_t_kernel(tc, x, child_h, child_c, Wf, bWf, Uf, 
                 if r == 0 and n == 2:
                     children[2] = quantise_rows(grouped.pop(2), child_codes_pool)
                 multiply(products, TWO * i + j, gates[(j, i)], cells[(j, i)])
-                if last_run and i == 0:
-                    cols = slice(j * BLOCK_COLUMNS, (j + 1) * BLOCK_COLUMNS)
-                    nc.gpsimd.tensor_tensor(out=total[:, cols], in0=total[:, cols], in1=first_child[:, cols], op=ADD)
             if "node" in grouped:
                 nodes[b + 1] = quantise_rows(grouped["node"], node_codes_pool)
             for s in prepare:
@@ -396,10 +393,12 @@ def tile_childsumtreelstmcell_pa_t_kernel(tc, x, child_h, child_c, Wf, bWf, Uf, 
             if ends_kernel:
                 for j in range(TWO):
                     cols = slice(j * BLOCK_COLUMNS, (j + 1) * BLOCK_COLUMNS)
-                    terms = [total[:, cols], (second_child if last_run else first_child)[:, cols]]
+                    terms = [total[:, cols], first_child[:, cols]]
+                    if last_run:
+                        terms.append(second_child[:, cols])
                     pending.append((TWO * half + j, terms))
 
         for hb, terms in pending:
-            keep_clock_up(2)
+            keep_clock_up(1)
             for half in range(TILES // 2):
                 store_half(BLOCKS - 1, hb, half, terms, "scalar" if hb < TWO or half == 0 else "vector")

from contextlib import ExitStack

import concourse.mybir as mybir
from concourse.masks import make_identity

F32 = mybir.dt.float32
BF16 = mybir.dt.bfloat16
U32 = mybir.dt.uint32
U8 = mybir.dt.uint8
FP8X4 = mybir.dt.float8_e4m3fn_x4
SIGMOID = mybir.ActivationFunctionType.Sigmoid
MULT = mybir.AluOpType.mult
ADD = mybir.AluOpType.add

P = 128
PACK = 4
NODES, CHILDREN, FEATURES, HIDDEN = 1024, 8, 512, 1024
FLOPS = 2 * (NODES * CHILDREN + NODES) * FEATURES * HIDDEN

NODE_BLOCK = 512
BLOCKS = NODES // NODE_BLOCK
TILES = NODE_BLOCK // P
PAIR = 2
WORDS = FEATURES // PAIR
HALVES = WORDS // P
H_BLOCK = PAIR * P
H_BLOCKS = HIDDEN // H_BLOCK
W_BOUNDS = (0, 2 * H_BLOCK, HIDDEN)
CELL_BANKS = 4
OTHER_BANKS = 4
TWO = 2
RUNS_PER_PAIR = H_BLOCKS // TWO
RUNS_PER_BLOCK = CHILDREN // TWO * RUNS_PER_PAIR
RUNS = BLOCKS * RUNS_PER_BLOCK
STEPS = BLOCKS * CHILDREN
BLOCK_COLUMNS = PAIR * NODE_BLOCK
RUN_COLUMNS = TWO * BLOCK_COLUMNS
RUN_ORDER = (
    [(0, pair, half) for half in range(TWO) for pair in range(TWO)]
    + [(0, pair, half) for pair in range(TWO, CHILDREN // TWO) for half in range(TWO)]
    + [(b, pair, half) for b in range(1, BLOCKS) for pair in range(CHILDREN // TWO) for half in range(TWO)]
)
STORE_RUN = 3
X_RUN = 3


def tile_childsumtreelstmcell_pa_t_kernel(tc, x, child_h, child_c, Wf, bWf, Uf, bUf, out):
    nc = tc.nc
    x_view = x.rearrange("(b p t) d -> b p (t d)", b=BLOCKS, t=TILES)
    h_view = child_h.rearrange("(b p t) (q i) d -> b p t q (i d)", b=BLOCKS, t=TILES, i=TWO)
    c_view = child_c.rearrange("(b p t) k h -> b p t k h", b=BLOCKS, t=TILES)
    out_view = out.rearrange("(b p t) h -> b p t h", b=BLOCKS, t=TILES)

    with ExitStack() as ctx:
        const = ctx.enter_context(tc.tile_pool(name="const", bufs=1))
        weights = ctx.enter_context(tc.tile_pool(name="weights", bufs=1))
        wstage = ctx.enter_context(tc.tile_pool(name="wstage", bufs=4))
        x_rows_pool = ctx.enter_context(tc.tile_pool(name="x_rows", bufs=1))
        h_rows_pool = ctx.enter_context(tc.tile_pool(name="h_rows", bufs=3))
        ordered_pool = ctx.enter_context(tc.tile_pool(name="ordered", bufs=2))
        c_rows_pool = ctx.enter_context(tc.tile_pool(name="c_rows", bufs=6))
        grouped_pool = ctx.enter_context(tc.tile_pool(name="grouped", bufs=3))
        child_codes_pool = ctx.enter_context(tc.tile_pool(name="child_codes", bufs=6))
        node_codes_pool = ctx.enter_context(tc.tile_pool(name="node_codes", bufs=BLOCKS))
        gate_pool = ctx.enter_context(tc.tile_pool(name="gate", bufs=6))
        prod_pool = ctx.enter_context(tc.tile_pool(name="prod", bufs=3))
        sum_pool = ctx.enter_context(tc.tile_pool(name="sums", bufs=BLOCKS))
        half_pool = ctx.enter_context(tc.tile_pool(name="half_rows", bufs=6))
        banks_pool = ctx.enter_context(tc.psum_pool(name="banks", bufs=OTHER_BANKS))
        cells_pool = ctx.enter_context(tc.psum_pool(name="cells", bufs=CELL_BANKS))
        ctx.enter_context(tc.manual_schedule())

        def load_weight_part(w, name, part):
            cols = slice(W_BOUNDS[part], W_BOUNDS[part + 1])
            last = part == len(W_BOUNDS) - 2
            pool, tag = (c_rows_pool, "c_rows") if last else (weights, "raw_%s%d" % (name, part))
            raw = pool.tile([P, PACK * (cols.stop - cols.start)], BF16, name="raw", tag=tag)
            nc.sync.dma_start(
                out=raw[:].rearrange("q (j c) -> q j c", j=PACK),
                in_=w[:, cols].rearrange("(q j) c -> q j c", j=PACK),
            )
            return raw

        def regroup_weight_block(raw_parts, hb):
            part = hb // TWO
            first = H_BLOCK * hb - W_BOUNDS[part]
            grouped_w = wstage.tile([P, H_BLOCK * PACK], BF16, align_bytes=64)
            grouped_view = grouped_w[:].rearrange("q (e m j) -> q e m j", e=PAIR, j=PACK)
            raw_view = raw_parts[part][:].rearrange("q (j c) -> q j c", j=PACK)[:, :, first : first + H_BLOCK].rearrange(
                "q j (m e) -> q e m j", e=PAIR
            )
            nc.vector.tensor_copy(out=grouped_view, in_=raw_view)
            return grouped_w

        def quantise_weight_block(grouped_w, codes, scales, hb):
            cols = slice(H_BLOCK * hb, H_BLOCK * (hb + 1))
            nc.vector.quantize_mx(out=codes[:, cols].bitcast(FP8X4), scales=scales[:, cols], in_=grouped_w[:])

        def load_x(b):
            rows = x_rows_pool.tile([P, TILES * FEATURES], BF16, name="x_rows")
            nc.sync.dma_start(out=rows[:], in_=x_view[b])
            return rows[:].bitcast(F32).rearrange("p (t w) -> p t w", t=TILES)

        def load_child_pair(s):
            b, k = divmod(s, CHILDREN)
            rows = h_rows_pool.tile([P, TILES * TWO * FEATURES], BF16, name="h_rows")
            nc.sync.dma_start(out=rows[:].rearrange("p (t f) -> p t f", t=TILES), in_=h_view[b, :, :, k // TWO, :])
            words = rows[:].bitcast(F32).rearrange("p (t i w) -> p t i w", t=TILES, i=TWO)
            for i in range(TWO):
                h_rows[s + i] = words[:, :, i, :]

        def load_cells(r):
            b, pair, half = RUN_ORDER[r]
            rows = []
            for k in (TWO * pair, TWO * pair + 1):
                cells = c_rows_pool.tile([P, TILES * TWO * H_BLOCK], BF16, name="c_rows", tag="c_rows")
                nc.sync.dma_start(
                    out=cells[:].rearrange("p (t h) -> p t h", t=TILES),
                    in_=c_view[b, :, :, k, TWO * H_BLOCK * half : TWO * H_BLOCK * (half + 1)],
                )
                rows.append(cells)
            return rows

        def transpose_rows(words, ordered=False):
            banks = []
            for half in range(TILES // 2):
                bank = banks_pool.tile([P, 2, HALVES, P], F32, name="bank", tag="bank")
                for a in range(2):
                    for u in range(HALVES):
                        taken = slice(u * P, (u + 1) * P) if ordered else slice(u, WORDS, HALVES)
                        nc.tensor.transpose(bank[:, a, u, :], words[:, 2 * half + a, taken], ident[:])
                banks.append(bank)
            return banks

        def order_words(words):
            ordered = ordered_pool.tile([P, TILES * FEATURES], BF16, name="ordered")
            nc.scalar.copy(
                out=ordered[:].bitcast(F32).rearrange("p (t u w) -> p t u w", t=TILES, u=HALVES),
                in_=words.rearrange("p t (w u) -> p t u w", u=HALVES),
            )
            return ordered[:].bitcast(F32).rearrange("p (t w) -> p t w", t=TILES)

        def regroup_rows(banks):
            grouped = grouped_pool.tile([P, NODE_BLOCK * PACK], BF16, align_bytes=64)
            grouped_words = grouped[:].bitcast(F32).rearrange("p (h a n u) -> p h a n u", h=2, a=2, u=HALVES)
            for half in range(TILES // 2):
                nc.scalar.copy(out=grouped_words[:, half], in_=banks[half][:].rearrange("p a u n -> p a n u"))
            return grouped

        def quantise_rows(grouped, pool):
            codes = pool.tile([P, NODE_BLOCK], U32, name="codes", align_bytes=64)
            scales = pool.tile([P, NODE_BLOCK], U8, name="scales", align_bytes=64)
            nc.vector.quantize_mx(out=codes[:].bitcast(FP8X4), scales=scales[:], in_=grouped[:])
            return codes, scales

        def gate_sums(hb, e, child, node):
            z = banks_pool.tile([P, NODE_BLOCK], F32, name="z", tag="bank")
            cols = slice((PAIR * hb + e) * P, (PAIR * hb + e + 1) * P)
            nc.tensor.matmul_mx(
                out=z[:],
                lhsT=u_codes[:, cols].bitcast(FP8X4),
                lhsT_scale=u_scales[:, cols],
                rhs=child[0][:].bitcast(FP8X4),
                rhs_scale=child[1][:],
                start=True,
                stop=False,
            )
            nc.tensor.matmul_mx(
                out=z[:],
                lhsT=w_codes[:, cols].bitcast(FP8X4),
                lhsT_scale=w_scales[:, cols],
                rhs=node[0][:].bitcast(FP8X4),
                rhs_scale=node[1][:],
                start=False,
                stop=True,
            )
            return z

        def transpose_cells(rows, j):
            words = rows[:].bitcast(F32)
            cells = cells_pool.tile([P, NODE_BLOCK], F32, name="cells", tag="cells")
            for t in range(TILES):
                first = (TWO * t + j) * P
                nc.tensor.transpose(cells[:, t * P : (t + 1) * P], words[:, first : first + P], ident[:])
            return cells

        def multiply(products, unit, gate, cells):
            nc.vector.tensor_tensor(
                out=products[:, unit * BLOCK_COLUMNS : (unit + 1) * BLOCK_COLUMNS].rearrange("p (e n) -> p e n", e=PAIR),
                in0=gate[:].rearrange("p (e n) -> p e n", e=PAIR),
                in1=cells[:].bitcast(BF16).rearrange("p (n e) -> p e n", e=PAIR),
                op=MULT,
            )

        def store_half(b, hb, half, terms, engine="scalar"):
            rows = half_pool.tile([P, TILES // 2 * H_BLOCK], F32, name="half_rows")
            bank = banks_pool.tile([P, 2, PAIR, P], F32, name="bank", tag="bank")
            for a in range(2):
                for e in range(PAIR):
                    first = e * NODE_BLOCK + (2 * half + a) * P
                    for i, term in enumerate(terms):
                        nc.tensor.matmul(
                            bank[:, a, e, :],
                            lhsT=term[:, first : first + P],
                            rhs=ident[:],
                            start=i == 0,
                            stop=i == len(terms) - 1,
                            is_transpose=True,
                        )
            rows_view = rows[:].rearrange("p (a w e) -> p a w e", a=2, e=PAIR)
            bank_view = bank[:].rearrange("p a e w -> p a w e")
            if engine == "scalar":
                nc.scalar.copy(out=rows_view, in_=bank_view)
            else:
                nc.vector.tensor_copy(out=rows_view, in_=bank_view)
            nc.sync.dma_start(
                out=out_view[b, :, 2 * half : 2 * half + 2, H_BLOCK * hb : H_BLOCK * (hb + 1)],
                in_=rows[:].rearrange("p (t h) -> p t h", t=TILES // 2),
            )

        def sum_columns(hb):
            return slice(hb * BLOCK_COLUMNS, (hb + 1) * BLOCK_COLUMNS)

        ident = const.tile([P, P], F32)
        make_identity(nc, ident[:])

        bias_rows = const.tile([P, P], F32)
        nc.vector.memset(bias_rows[:], 0.0)
        bias_rows_bf = bias_rows[:].bitcast(BF16)

        def load_biases():
            nc.sync.dma_start(out=bias_rows_bf[0:H_BLOCKS, :], in_=bWf.rearrange("(r c) -> r c", c=H_BLOCK))
            nc.sync.dma_start(out=bias_rows_bf[H_BLOCKS : 2 * H_BLOCKS, :], in_=bUf.rearrange("(r c) -> r c", c=H_BLOCK))

        zeros = const.tile([P, NODE_BLOCK], BF16)
        nc.vector.memset(zeros[:], 0.0)

        def keep_clock_up(count):
            unused = banks_pool.tile([P, NODE_BLOCK], F32, name="unused", tag="bank")
            for n in range(count):
                nc.tensor.matmul(unused[:], lhsT=zeros[:, 0:P], rhs=zeros[:], start=True, stop=True)

        first_sigmoid = const.tile([P, 1], F32)
        nc.vector.memset(first_sigmoid[:], 0.0)
        nc.scalar.activation(out=first_sigmoid[:], in_=first_sigmoid[:], func=SIGMOID)

        u_raw = {}
        w_raw = {}
        h_rows = {}
        x_rows = {}
        c_rows = {}
        load_child_pair(0)
        load_biases()
        x_rows[0] = load_x(0)
        u_raw[0] = load_weight_part(Uf, "u", 0)
        w_raw[0] = load_weight_part(Wf, "w", 0)
        c_rows[0] = load_cells(0)
        load_child_pair(2)
        c_rows[1] = load_cells(1)
        u_raw[1] = load_weight_part(Uf, "u", 1)
        w_raw[1] = load_weight_part(Wf, "w", 1)
        load_child_pair(4)
        c_rows[2] = load_cells(2)
        x_rows[1] = load_x(1)

        u_codes = weights.tile([P, HIDDEN], U32, align_bytes=64)
        u_scales = weights.tile([P, HIDDEN], U8, align_bytes=64)
        w_codes = weights.tile([P, HIDDEN], U32, align_bytes=64)
        w_scales = weights.tile([P, HIDDEN], U8, align_bytes=64)

        keep_clock_up(12)
        banks_h0 = transpose_rows(h_rows[0])
        keep_clock_up(2)
        banks_x0 = transpose_rows(x_rows[0])
        keep_clock_up(2)
        grouped_h0 = regroup_rows(banks_h0)
        grouped_x0 = regroup_rows(banks_x0)
        grouped_u = regroup_weight_block(u_raw, 0)
        children = {0: quantise_rows(grouped_h0, child_codes_pool)}
        quantise_weight_block(grouped_u, u_codes, u_scales, 0)
        grouped_w = regroup_weight_block(w_raw, 0)
        nodes = {0: quantise_rows(grouped_x0, node_codes_pool)}
        quantise_weight_block(grouped_w, w_codes, w_scales, 0)

        bias_ps = banks_pool.tile([P, P], F32, name="bias_ps", tag="bank")
        nc.tensor.transpose(bias_ps[:], bias_rows[:], ident[:])
        grouped_h1 = regroup_rows(transpose_rows(h_rows[1]))
        keep_clock_up(1)
        both = const.tile([P, 2 * PAIR * H_BLOCKS], F32)
        nc.vector.tensor_copy(out=both[:], in_=bias_ps[:, 0 : 2 * H_BLOCKS].bitcast(BF16))
        bias = const.tile([P, PAIR * H_BLOCKS], F32)
        nc.vector.tensor_tensor(
            out=bias[:], in0=both[:, 0 : PAIR * H_BLOCKS], in1=both[:, PAIR * H_BLOCKS : 2 * PAIR * H_BLOCKS], op=ADD
        )
        grouped_u = regroup_weight_block(u_raw, 1)
        children[1] = quantise_rows(grouped_h1, child_codes_pool)
        grouped_w = regroup_weight_block(w_raw, 1)
        quantise_weight_block(grouped_u, u_codes, u_scales, 1)
        quantise_weight_block(grouped_w, w_codes, w_scales, 1)
        def prepare_weight_block(hb):
            grouped_u = regroup_weight_block(u_raw, hb)
            grouped_w = regroup_weight_block(w_raw, hb)
            quantise_weight_block(grouped_u, u_codes, u_scales, hb)
            quantise_weight_block(grouped_w, w_codes, w_scales, hb)

        sums = {}
        ordered_rows = {}
        pending = []

        for r in range(RUNS):
            b, pair, half = RUN_ORDER[r]
            first_step = b * CHILDREN + TWO * pair
            units = [(j, i) for j in range(TWO) for i in range(TWO)]
            if r == 1:
                units = [(j, i) for i in range(TWO) for j in range(TWO)]
            prepare = [2, 3] if r == 0 else [r + 3]
            last_run = r == RUNS - 1
            if r % TWO == 0 and r + 6 < STEPS:
                load_child_pair(r + 6)
            if r + 2 < RUNS and r + 2 not in c_rows:
                c_rows[r + 2] = load_cells(r + 2)

            z = {}
            cells = {}
            gates = {}
            grouped = {}
            groups = [units[:2], units[2:]] if last_run or r == 0 else [units]
            for g, group in enumerate(groups):
                for j, i in group:
                    for e in range(PAIR):
                        z[(j, i, e)] = gate_sums(TWO * half + j, e, children[first_step + i], nodes[b])
                for j, i in group:
                    cells[(j, i)] = transpose_cells(c_rows[r][i], j)
                for j, i in group:
                    gate = gate_pool.tile([P, BLOCK_COLUMNS], F32)
                    for e in range(PAIR):
                        hb = TWO * half + j
                        nc.scalar.activation(
                            out=gate[:, e * NODE_BLOCK : (e + 1) * NODE_BLOCK],
                            in_=z[(j, i, e)][:],
                            func=SIGMOID,
                            bias=bias[:, PAIR * hb + e : PAIR * hb + e + 1],
                            scale=1.0,
                        )
                    gates[(j, i)] = gate

                if r == 0 and g == 0:
                    grouped[2] = regroup_rows(transpose_rows(h_rows[2]))

            if r >= 1 and r + 4 < STEPS:
                ordered_rows[r + 4] = order_words(h_rows[r + 4])
            for s in prepare:
                if s < STEPS and s not in grouped:
                    in_order = s in ordered_rows
                    grouped[s] = regroup_rows(transpose_rows(ordered_rows[s] if in_order else h_rows[s], in_order))
            if r % RUNS_PER_BLOCK == X_RUN and b + 1 < BLOCKS:
                grouped["node"] = regroup_rows(transpose_rows(x_rows[b + 1]))

            out_hb = r - RUNS_PER_BLOCK - STORE_RUN
            if 0 <= out_hb < H_BLOCKS:
                for n in range(TILES // 2):
                    store_half(b - 1, out_hb, n, [sums[b - 1][:, sum_columns(out_hb)]])

            if r % RUNS_PER_BLOCK == 0:
                sums[b] = sum_pool.tile([P, H_BLOCKS * BLOCK_COLUMNS], F32, name="total")
            products = prod_pool.tile([P, TWO * RUN_COLUMNS], F32, name="products", tag="products")
            first_child, second_child = products[:, 0:RUN_COLUMNS], products[:, RUN_COLUMNS : 2 * RUN_COLUMNS]
            total = sums[b][:, half * RUN_COLUMNS : (half + 1) * RUN_COLUMNS]
            for n, (j, i) in enumerate(units):
                if r == 0 and n == 2:
                    children[2] = quantise_rows(grouped.pop(2), child_codes_pool)
                multiply(products, TWO * i + j, gates[(j, i)], cells[(j, i)])
            if "node" in grouped:
                nodes[b + 1] = quantise_rows(grouped["node"], node_codes_pool)
            for s in prepare:
                if s in grouped:
                    children[s] = quantise_rows(grouped[s], child_codes_pool)
            if r == 0:
                for hb in range(TWO, H_BLOCKS):
                    prepare_weight_block(hb)
            ends_kernel = r >= RUNS - RUNS_PER_PAIR
            if pair == 0:
                if b == 0:
                    nc.vector.memset(total[:, 0:1], 0.0)
                nc.gpsimd.tensor_tensor(out=total, in0=first_child, in1=second_child, op=ADD)
            elif not last_run:
                parts = 1 if prepare[0] < STEPS else TWO
                for j in range(parts):
                    cols = slice(j * RUN_COLUMNS // parts, (j + 1) * RUN_COLUMNS // parts)
                    nc.vector.tensor_tensor(out=first_child[:, cols], in0=first_child[:, cols], in1=second_child[:, cols], op=ADD)
                if not ends_kernel:
                    nc.gpsimd.tensor_tensor(out=total, in0=total, in1=first_child, op=ADD)
            if ends_kernel:
                for j in range(TWO):
                    cols = slice(j * BLOCK_COLUMNS, (j + 1) * BLOCK_COLUMNS)
                    terms = [total[:, cols], first_child[:, cols]]
                    if last_run:
                        terms.append(second_child[:, cols])
                    pending.append((TWO * half + j, terms))

        for hb, terms in pending:
            keep_clock_up(1)
            for half in range(TILES // 2):
                store_half(BLOCKS - 1, hb, half, terms, "scalar" if hb < TWO or half == 0 else "vector")
